import numpy as np
import ml_dtypes


def mxq(x, axis, fmt="e4m3"):
    dtype, down = {"e4m3": (ml_dtypes.float8_e4m3fn, 7), "e5m2": (ml_dtypes.float8_e5m2, 14)}[fmt]
    v = np.moveaxis(np.asarray(x, np.float32).astype(ml_dtypes.bfloat16).astype(np.float64), axis, -1)
    blocks = v.reshape(v.shape[:-1] + (-1, 32))
    amax = np.abs(blocks).max(-1, keepdims=True)
    byte = np.maximum(np.where(amax > 0, np.frexp(amax)[1] - 1 + 127, 0) - down, 1)
    scale = np.exp2(byte - 127.0)
    codes = (blocks / scale).astype(np.float32).astype(dtype).astype(np.float64)
    return np.moveaxis((codes * scale).reshape(v.shape), -1, axis)


WIDE = False


def mx_kscale(k):
    if not WIDE:
        return np.ones(k)
    levels = np.array([10, -10, 5, -5, 0])
    a = np.random.permutation(np.resize(levels, k // 512 * 4)).reshape(k // 512, 4)
    idx = np.arange(k)
    return np.exp2(a[idx // 512, idx % 128 // 32])


BF16 = ml_dtypes.bfloat16


def bf(x):
    return np.asarray(x, np.float32).astype(BF16)


def f64(x):
    return np.asarray(x).astype(np.float64)


B, DIM, HID, H, SEQ, DOUT = 512, 2048, 256, 8, 2048, 2048
DECAY_CONSTANT = SEQ // 512
H2 = H // 2
F = H * HID


def setup_inputs():
    s = mx_kscale(DIM)
    x = bf(np.random.standard_normal((B, DIM)) * s)
    W_proj = bf(np.random.standard_normal((H, DIM, HID)) / np.sqrt(DIM) / s[:, None])
    b_proj = bf(np.random.standard_normal((H, HID)) * 0.1)
    W_out = bf(np.random.standard_normal((F, DOUT)) / np.sqrt(F))
    b_out = bf(np.random.standard_normal(DOUT) * 0.1)
    w_mix = bf(np.concatenate([0.4 + 0.05 * np.random.standard_normal((H2, SEQ)), -0.3 + 0.05 * np.random.standard_normal((H - H2, SEQ))], axis=0))
    b_mix = bf(np.concatenate([3.0 + 0.1 * np.random.standard_normal((H2, SEQ)), 0.2 + 0.1 * np.random.standard_normal((H - H2, SEQ))], axis=0))
    decay_values = bf(0.95 + 0.05 * np.random.standard_normal(H))
    caches = bf(np.random.standard_normal((H, B, HID)))
    return {"x": x, "index": 7, "W_proj": W_proj, "b_proj": b_proj, "W_out": W_out, "b_out": b_out,
            "w_mix": w_mix, "b_mix": b_mix, "decay_values": decay_values, "caches": caches}


def reference(x, index, W_proj, b_proj, W_out, b_out, w_mix, b_mix, decay_values, caches):
    proj = (mxq(f64(x), 1, "e4m3") @ mxq(f64(W_proj), 1, "e4m3")) + f64(b_proj)[:, None, :]
    decay = np.clip(f64(decay_values), 0.9, 1.0) ** (1.0 / DECAY_CONSTANT)
    w = f64(w_mix)[:, index]
    b = f64(b_mix)[:, index]
    cache_coef = np.concatenate([w[:H2] * decay[:H2], decay[H2:]], axis=0)
    out = (w[:, None, None] * proj
           + cache_coef[:, None, None] * f64(caches)
           + b[:, None, None])
    hidden = np.transpose(out, (1, 0, 2)).reshape(B, H * HID)
    return (mxq(hidden, 1, "e4m3") @ mxq(f64(W_out), 0, "e4m3")) + f64(b_out)

@@ -1,0 +1,428 @@
+from contextlib import ExitStack
+
+import concourse.masks as masks
+import concourse.mybir as mybir
+
+F32 = mybir.dt.float32
+BF16 = mybir.dt.bfloat16
+U32 = mybir.dt.uint32
+U8 = mybir.dt.uint8
+FP8X4 = mybir.dt.float8_e4m3fn_x4
+ALU = mybir.AluOpType
+ACT = mybir.ActivationFunctionType
+
+P = 128
+FLOPS = 2 * 512 * 2048 * 2048 * 2
+
+RAW_BUFS = 8
+WOUT_V_COLS = (160, 160, 160, 160)
+
+
+def tile_mixedrepeatheads_kernel(
+    tc, x, index, W_proj, b_proj, W_out, b_out, w_mix, b_mix, decay_values, caches, out
+):
+    nc = tc.nc
+    with ExitStack() as ctx:
+        ctx.enter_context(tc.manual_schedule())
+        const = ctx.enter_context(tc.tile_pool(name="const", bufs=1))
+        rawp = ctx.enter_context(tc.tile_pool(name="rawp", bufs=RAW_BUFS))
+        grpp = ctx.enter_context(tc.tile_pool(name="grpp", bufs=6))
+        cachep = ctx.enter_context(tc.tile_pool(name="cachep", bufs=4))
+        wqp = ctx.enter_context(tc.tile_pool(name="wqp", bufs=2))
+        ctpp = ctx.enter_context(tc.tile_pool(name="ctpp", bufs=2))
+        outp = ctx.enter_context(tc.tile_pool(name="outp", bufs=2))
+        psum = ctx.enter_context(tc.psum_pool(name="psum", bufs=8))
+
+        bo = const.tile([P, 2048], BF16)
+        plan = [("wp", 0, 0), ("wp", 1, 0), ("x", 0, 0), ("x", 1, 0), ("c", 0, 0)]
+        for G in range(1, 4):
+            plan.append(("wp", 2 * G, 0))
+            plan.append(("wp", 2 * G + 1, 0))
+            plan.append(("c", G, 0))
+        plan.append(("bo", 0, 0))
+        for half in range(2):
+            for G in range(4):
+                plan.append(("wo", half, G))
+        state = {"pos": 0, "raw": 0, "done": 0}
+        tiles = {}
+        xview = x.rearrange("(p r) k -> p r k", r=4)
+
+        def wp_view(h):
+            return W_proj[h].rearrange("(g p j) c -> p g (j c)", g=4, p=P, j=4)
+
+        def issue(kind, a, b):
+            if kind == "x":
+                t = rawp.tile([P, 4096], BF16, tag="raw")
+                nc.sync.dma_start(
+                    out=t[:].rearrange("p (r k) -> p r k", r=2), in_=xview[:, 2 * a : 2 * a + 2, :]
+                )
+                tiles[(kind, a, b)] = t
+            elif kind == "wp":
+                t = rawp.tile([P, 4096], BF16, tag="raw")
+                tiles[(kind, a, b)] = t
+                if a >= 2:
+                    nc.sync.dma_start(out=t[:].rearrange("p (g e) -> p g e", g=4), in_=wp_view(a))
+                elif a == 1:
+                    for g in range(4):
+                        for h in range(2):
+                            nc.sync.dma_start(
+                                out=tiles[("wp", h, 0)][:, g * 1024 : g * 1024 + 1024],
+                                in_=wp_view(h)[:, g, :],
+                            )
+            elif kind == "wo":
+                t = rawp.tile([P, 4096], BF16, tag="raw")
+                nc.sync.dma_start(
+                    out=t[:].rearrange("p (j n) -> p j n", j=4),
+                    in_=W_out[512 * b : 512 * b + 512, 1024 * a : 1024 * a + 1024].rearrange(
+                        "(p j) n -> p j n", j=4
+                    ),
+                )
+                tiles[(kind, a, b)] = t
+            elif kind == "c":
+                t = cachep.tile([P, 2048], BF16, tag="craw")
+                tv = t[:].rearrange("p (r c) -> p r c", r=4)
+                for u in range(2):
+                    nc.sync.dma_start(
+                        out=tv[:, :, 256 * u : 256 * u + 256],
+                        in_=caches[2 * a + u].rearrange("(p r) c -> p r c", r=4),
+                    )
+                tiles[(kind, a, b)] = t
+            else:
+                nc.sync.dma_start(out=bo[:], in_=b_out.partition_broadcast(P))
+
+        def fetch(raw_count):
+            while state["pos"] < len(plan):
+                kind, a, b = plan[state["pos"]]
+                is_raw = kind in ("x", "wp", "wo")
+                if is_raw and state["raw"] >= raw_count:
+                    break
+                issue(kind, a, b)
+                state["pos"] += 1
+                if is_raw:
+                    state["raw"] += 1
+
+        def retire(count):
+            state["done"] += count
+            fetch(state["done"] + RAW_BUFS)
+
+        fetch(RAW_BUFS)
+
+        warm = const.tile([P, 1], F32)
+        nc.vector.memset(warm[:], 1.0)
+        nc.scalar.sqrt(warm[:], warm[:])
+
+        ident = const.tile([P, P], F32)
+        masks.make_identity(nc, ident[:])
+
+        wv = const.tile([P, 4], BF16)
+        bv = const.tile([P, 4], BF16)
+        dv = const.tile([P, 4], BF16)
+        bp = const.tile([P, 4, 4], BF16)
+        with nc.allow_non_contiguous_dma(reason="a few per-head scalars"):
+            for u in range(2):
+                rows = slice(64 * u, 64 * u + 64)
+                nc.scalar.dma_start(
+                    out=wv[rows, :],
+                    in_=w_mix[:, index].rearrange("(g u) -> u g", u=2)[u].partition_broadcast(64),
+                )
+                nc.scalar.dma_start(
+                    out=bv[rows, :],
+                    in_=b_mix[:, index].rearrange("(g u) -> u g", u=2)[u].partition_broadcast(64),
+                )
+                nc.scalar.dma_start(
+                    out=dv[rows, :],
+                    in_=decay_values.rearrange("(g u) -> u g", u=2)[u].partition_broadcast(64),
+                )
+            nc.scalar.dma_start(
+                out=bp[:],
+                in_=b_proj.rearrange("h c -> (h c)").rearrange("(g p t) -> p g t", p=P, t=4),
+            )
+
+        w32 = const.tile([P, 4], F32)
+        b32 = const.tile([P, 4], F32)
+        dclip = const.tile([P, 4], F32)
+        droot = const.tile([P, 4], F32)
+        decay = const.tile([P, 4], F32)
+        coef = const.tile([P, 4], F32)
+        bias = const.tile([P, 4, 4], F32)
+
+        def small_vectors():
+            nc.vector.tensor_copy(out=w32[:], in_=wv[:])
+            nc.vector.tensor_copy(out=b32[:], in_=bv[:])
+            nc.vector.tensor_scalar(
+                out=dclip[:], in0=dv[:], scalar1=0.9, scalar2=1.0, op0=ALU.max, op1=ALU.min
+            )
+            nc.scalar.sqrt(droot[:], dclip[:])
+            nc.scalar.sqrt(decay[:], droot[:])
+            for G in range(4):
+                nc.vector.tensor_scalar(
+                    out=bias[:, G, :],
+                    in0=bp[:, G, :],
+                    scalar1=w32[:, G : G + 1],
+                    scalar2=b32[:, G : G + 1],
+                    op0=ALU.mult,
+                    op1=ALU.add,
+                )
+            nc.vector.tensor_mul(coef[:, 0:2], w32[:, 0:2], decay[:, 0:2])
+            nc.vector.tensor_copy(out=coef[:, 2:4], in_=decay[:, 2:4])
+
+        xc = const.tile([P, 4, 512], U32, align_bytes=64)
+        xs = const.tile([P, 4, 512], U8, align_bytes=64)
+        hc = const.tile([P, 4, 512], U32, align_bytes=64)
+        hs = const.tile([P, 4, 512], U8, align_bytes=64)
+        woc = const.tile([P, 16, 512], U32, align_bytes=64)
+        wos = const.tile([P, 16, 512], U8, align_bytes=64)
+
+        live = {}
+
+        def grp_tile(key):
+            if key not in live:
+                gt = grpp.tile([P, 2048], BF16, tag="grp", align_bytes=64)
+                live[key] = gt
+            return live[key]
+
+        def new_bank(key):
+            bank = psum.tile([P, 512], F32, tag="bank")
+            live[key] = bank
+            return bank
+
+        def copy_on(eng, dst, src):
+            if eng == 0:
+                nc.vector.tensor_copy(out=dst, in_=src)
+            else:
+                nc.scalar.copy(out=dst, in_=src)
+
+        def x_bank(rp, g):
+            xw = tiles[("x", rp, 0)][:].bitcast(F32)
+            bank = new_bank(("xb", rp, g))
+            for u in range(2):
+                for rl in range(2):
+                    base = rl * 1024 + 256 * g
+                    nc.tensor.transpose(
+                        bank[:, u * 256 + rl * 128 : u * 256 + rl * 128 + 128],
+                        xw[:, base + u : base + 256 : 2],
+                        ident[:],
+                    )
+            copy_on(
+                (g + 1) % 2,
+                grp_tile(("xg", g))[:].bitcast(F32).rearrange("q (r u) -> q r u", u=2)[
+                    :, rp * 256 : rp * 256 + 256, :
+                ],
+                bank[:].rearrange("q (u r) -> q r u", u=2),
+            )
+
+        def x_quant(g):
+            nc.vector.quantize_mx(
+                out=xc[:, g, :].bitcast(FP8X4), scales=xs[:, g, :], in_=grp_tile(("xg", g))[:]
+            )
+
+        def wp_regroup(G, g):
+            dst = grp_tile(("wg", G, g))[:].rearrange("p (t m j) -> p t m j", t=4, m=P, j=4)
+            for u in range(2):
+                src = tiles[("wp", 2 * G + u, 0)][:, g * 1024 : g * 1024 + 1024].rearrange(
+                    "p (j m t) -> p m j t", j=4, m=64, t=4
+                )
+                dstu = dst[:, :, 64 * u : 64 * u + 64, :].rearrange("p t m j -> p m j t")
+                copy_on((g + u) % 2, dstu, src)
+
+        def wp_quant(G, g):
+            if ("wpc", G) not in live:
+                wpc = wqp.tile([P, 4, 512], U32, tag="wpc", align_bytes=64)
+                wps = wqp.tile([P, 4, 512], U8, tag="wps", align_bytes=64)
+                live[("wpc", G)] = wpc
+                live[("wps", G)] = wps
+            nc.vector.quantize_mx(
+                out=live[("wpc", G)][:, g, :].bitcast(FP8X4),
+                scales=live[("wps", G)][:, g, :],
+                in_=grp_tile(("wg", G, g))[:],
+            )
+
+        def c_transpose(G, u2):
+            cw = tiles[("c", G, 0)][:].bitcast(F32).rearrange("p (r w) -> p r w", r=4)
+            bank = new_bank(("cb", G, u2))
+            for rr in range(4):
+                nc.tensor.transpose(
+                    bank[:, rr * 128 : rr * 128 + 128], cw[:, rr, u2 : 256 : 2], ident[:]
+                )
+
+        def c_scale(G):
+            ctp = ctpp.tile([P, 4, 512], F32, tag="ctp")
+            live[("ctp", G)] = ctp
+            for u2 in range(2):
+                bview = live[("cb", G, u2)][:].bitcast(BF16).rearrange("m (r e) -> m r e", e=2)
+                for e in range(2):
+                    t = 2 * u2 + e
+                    nc.scalar.activation(
+                        out=ctp[:, t, :],
+                        in_=bview[:, :, e],
+                        func=ACT.Identity,
+                        bias=bias[:, G, t : t + 1],
+                        scale=coef[:, G : G + 1],
+                    )
+
+        def m1(G, rr):
+            bank = new_bank(("mb", G, rr))
+            wpc = live[("wpc", G)]
+            wps = live[("wps", G)]
+            for t in range(4):
+                for g in range(4):
+                    nc.tensor.matmul_mx(
+                        out=bank[:, t * 128 : t * 128 + 128],
+                        lhsT=wpc[:, g, t * 128 : t * 128 + 128].bitcast(FP8X4),
+                        lhsT_scale=wps[:, g, t * 128 : t * 128 + 128],
+                        rhs=xc[:, g, rr * 128 : rr * 128 + 128].bitcast(FP8X4),
+                        rhs_scale=xs[:, g, rr * 128 : rr * 128 + 128],
+                        start=(g == 0),
+                        stop=(g == 3),
+                    )
+
+        def mix(G, rr):
+            nc.vector.scalar_tensor_tensor(
+                out=grp_tile(("hg", G))[:, rr * 512 : rr * 512 + 512].rearrange(
+                    "m (r t) -> m r t", t=4
+                ),
+                in0=live[("mb", G, rr)][:].rearrange("m (t r) -> m r t", t=4),
+                scalar=w32[:, G : G + 1],
+                in1=live[("ctp", G)][:, :, rr * 128 : rr * 128 + 128].rearrange("m t r -> m r t"),
+                op0=ALU.mult,
+                op1=ALU.add,
+            )
+
+        def h_quant(G):
+            nc.vector.quantize_mx(
+                out=hc[:, G, :].bitcast(FP8X4), scales=hs[:, G, :], in_=grp_tile(("hg", G))[:]
+            )
+
+        def wo_regroup(nb, G):
+            wr = tiles[("wo", nb // 2, G)][:].rearrange("p (j n) -> p j n", j=4)
+            off = (nb % 2) * 512
+            dst = grp_tile(("og", nb, G))[:].rearrange("p (n j) -> p n j", j=4)
+            cut = WOUT_V_COLS[nb]
+            for lo, hi, eng in ((0, cut, 0), (cut, 512, 1)):
+                copy_on(
+                    eng,
+                    dst[:, lo:hi, :].rearrange("p (c i) j -> p c j i", i=4),
+                    wr[:, :, off + lo : off + hi].rearrange("p j (c i) -> p c j i", i=4),
+                )
+
+        def wo_quant(nb, G):
+            nc.vector.quantize_mx(
+                out=woc[:, nb * 4 + G, :].bitcast(FP8X4),
+                scales=wos[:, nb * 4 + G, :],
+                in_=grp_tile(("og", nb, G))[:],
+            )
+
+        def m2(nb, G):
+            for rr in range(4):
+                if G == 0:
+                    new_bank(("ob", nb, rr))
+                nc.tensor.matmul_mx(
+                    out=live[("ob", nb, rr)][:],
+                    lhsT=hc[:, G, rr * 128 : rr * 128 + 128].bitcast(FP8X4),
+                    lhsT_scale=hs[:, G, rr * 128 : rr * 128 + 128],
+                    rhs=woc[:, nb * 4 + G, :].bitcast(FP8X4),
+                    rhs_scale=wos[:, nb * 4 + G, :],
+                    start=(G == 0),
+                    stop=(G == 3),
+                )
+
+        oview = out.rearrange("(p r) n -> p r n", r=4)
+
+        def add_bias(nb, rr):
+            if ("ost", nb) not in live:
+                ost = outp.tile([P, 4, 512], F32, tag="ost")
+                live[("ost", nb)] = ost
+            nc.vector.tensor_tensor(
+                out=live[("ost", nb)][:, rr, :],
+                in0=live[("ob", nb, rr)][:],
+                in1=bo[:, nb * 512 : nb * 512 + 512],
+                op=ALU.add,
+            )
+
+        def store(nb, r0, r1):
+            nc.sync.dma_start(
+                out=oview[:, r0:r1, nb * 512 : nb * 512 + 512], in_=live[("ost", nb)][:, r0:r1, :]
+            )
+
+        wp_regroup(0, 0)
+        wp_regroup(0, 1)
+        wp_quant(0, 0)
+        wp_regroup(0, 2)
+        wp_quant(0, 1)
+        wp_regroup(0, 3)
+        wp_quant(0, 2)
+        wp_quant(0, 3)
+        retire(2)
+        small_vectors()
+        for rp in range(2):
+            for g in range(4):
+                x_bank(rp, g)
+            retire(1)
+        for g in range(4):
+            x_quant(g)
+        c_transpose(0, 0)
+        c_transpose(0, 1)
+        c_scale(0)
+        for G in range(1, 4):
+            wp_regroup(G, 0)
+            wp_regroup(G, 1)
+            wp_quant(G, 0)
+            m1(G - 1, 0)
+            wp_regroup(G, 2)
+            wp_quant(G, 1)
+            mix(G - 1, 0)
+            m1(G - 1, 1)
+            wp_regroup(G, 3)
+            retire(2)
+            wp_quant(G, 2)
+            mix(G - 1, 1)
+            c_transpose(G, 0)
+            c_transpose(G, 1)
+            m1(G - 1, 2)
+            wp_quant(G, 3)
+            mix(G - 1, 2)
+            m1(G - 1, 3)
+            mix(G - 1, 3)
+            h_quant(G - 1)
+            c_scale(G)
+
+        def behind(nb, i):
+            if nb == 0:
+                m1(3, i)
+                mix(3, i)
+                if i == 3:
+                    h_quant(3)
+            else:
+                add_bias(nb - 1, i)
+                if i % 2 == 1:
+                    store(nb - 1, i - 1, i + 1)
+
+        for nb in range(4):
+            wo_regroup(nb, 0)
+            wo_regroup(nb, 1)
+            wo_quant(nb, 0)
+            if nb > 0:
+                m2(nb, 0)
+            behind(nb, 0)
+            wo_regroup(nb, 2)
+            wo_quant(nb, 1)
+            if nb > 0:
+                m2(nb, 1)
+            behind(nb, 1)
+            wo_regroup(nb, 3)
+            wo_quant(nb, 2)
+            if nb > 0:
+                m2(nb, 2)
+            behind(nb, 2)
+            wo_quant(nb, 3)
+            behind(nb, 3)
+            if nb == 0:
+                for G in range(4):
+                    m2(0, G)
+            else:
+                m2(nb, 3)
+            if nb % 2 == 1:
+                retire(4)
+        for rr in range(4):
+            add_bias(3, rr)
+            store(3, rr, rr + 1)

@@ -39,7 +39,6 @@ def tile_mixedrepeatheads_kernel(
             plan.append(("wp", 2 * G, 0))
             plan.append(("wp", 2 * G + 1, 0))
             plan.append(("c", G, 0))
-        plan.append(("bo", 0, 0))
         for half in range(2):
             for G in range(4):
                 plan.append(("wo", half, G))
@@ -63,12 +62,16 @@ def tile_mixedrepeatheads_kernel(
                 if a >= 2:
                     nc.sync.dma_start(out=t[:].rearrange("p (g e) -> p g e", g=4), in_=wp_view(a))
                 elif a == 1:
-                    for g in range(4):
+                    for g0, g1 in ((0, 1), (1, 4)):
                         for h in range(2):
                             nc.sync.dma_start(
-                                out=tiles[("wp", h, 0)][:, g * 1024 : g * 1024 + 1024],
-                                in_=wp_view(h)[:, g, :],
+                                out=tiles[("wp", h, 0)][:, g0 * 1024 : g1 * 1024].rearrange(
+                                    "p (g e) -> p g e", e=1024
+                                ),
+                                in_=wp_view(h)[:, g0:g1, :],
                             )
+                        if g0 == 0:
+                            row_loads()
             elif kind == "wo":
                 t = rawp.tile([P, 4096], BF16, tag="raw")
                 nc.sync.dma_start(
@@ -78,7 +81,7 @@ def tile_mixedrepeatheads_kernel(
                     ),
                 )
                 tiles[(kind, a, b)] = t
-            elif kind == "c":
+            else:
                 t = cachep.tile([P, 2048], BF16, tag="craw")
                 tv = t[:].rearrange("p (r c) -> p r c", r=4)
                 for u in range(2):
@@ -87,8 +90,6 @@ def tile_mixedrepeatheads_kernel(
                         in_=caches[2 * a + u].rearrange("(p r) c -> p r c", r=4),
                     )
                 tiles[(kind, a, b)] = t
-            else:
-                nc.sync.dma_start(out=bo[:], in_=b_out.partition_broadcast(P))
 
         def fetch(raw_count):
             while state["pos"] < len(plan):
@@ -105,38 +106,32 @@ def tile_mixedrepeatheads_kernel(
             state["done"] += count
             fetch(state["done"] + RAW_BUFS)
 
-        fetch(RAW_BUFS)
-
         warm = const.tile([P, 1], F32)
         nc.vector.memset(warm[:], 1.0)
         nc.scalar.sqrt(warm[:], warm[:])
 
+        rows0 = const.tile([P, 2112], BF16)
+        ones = const.tile([P, P], BF16)
+        nc.vector.memset(rows0[:].bitcast(F32), 0.0)
+        nc.vector.memset(ones[:], 1.0)
+
         ident = const.tile([P, P], F32)
         masks.make_identity(nc, ident[:])
 
-        wv = const.tile([P, 4], BF16)
-        bv = const.tile([P, 4], BF16)
-        dv = const.tile([P, 4], BF16)
         bp = const.tile([P, 4, 4], BF16)
-        with nc.allow_non_contiguous_dma(reason="a few per-head scalars"):
-            for u in range(2):
-                rows = slice(64 * u, 64 * u + 64)
-                nc.scalar.dma_start(
-                    out=wv[rows, :],
-                    in_=w_mix[:, index].rearrange("(g u) -> u g", u=2)[u].partition_broadcast(64),
-                )
-                nc.scalar.dma_start(
-                    out=bv[rows, :],
-                    in_=b_mix[:, index].rearrange("(g u) -> u g", u=2)[u].partition_broadcast(64),
-                )
-                nc.scalar.dma_start(
-                    out=dv[rows, :],
-                    in_=decay_values.rearrange("(g u) -> u g", u=2)[u].partition_broadcast(64),
-                )
-            nc.scalar.dma_start(
-                out=bp[:],
-                in_=b_proj.rearrange("h c -> (h c)").rearrange("(g p t) -> p g t", p=P, t=4),
-            )
+        nc.sync.dma_start(
+            out=bp[:],
+            in_=b_proj.rearrange("h c -> (h c)").rearrange("(g p t) -> p g t", p=P, t=4),
+        )
+
+        def row_loads():
+            with nc.allow_non_contiguous_dma(reason="a few per-head scalars"):
+                nc.sync.dma_start(out=rows0[0:1, 2048:2056], in_=w_mix[:, index].unsqueeze(0))
+                nc.sync.dma_start(out=rows0[0:1, 2064:2072], in_=b_mix[:, index].unsqueeze(0))
+                nc.sync.dma_start(out=rows0[0:1, 2080:2088], in_=decay_values.unsqueeze(0))
+            nc.sync.dma_start(out=rows0[0:1, 0:2048], in_=b_out.unsqueeze(0))
+
+        fetch(RAW_BUFS)
 
         w32 = const.tile([P, 4], F32)
         b32 = const.tile([P, 4], F32)
@@ -147,11 +142,22 @@ def tile_mixedrepeatheads_kernel(
         bias = const.tile([P, 4, 4], F32)
 
         def small_vectors():
-            nc.vector.tensor_copy(out=w32[:], in_=wv[:])
-            nc.vector.tensor_copy(out=b32[:], in_=bv[:])
-            nc.vector.tensor_scalar(
-                out=dclip[:], in0=dv[:], scalar1=0.9, scalar2=1.0, op0=ALU.max, op1=ALU.min
+            heads = psum.tile([P, 512], F32, tag="bank")
+            nc.tensor.matmul(
+                out=heads[:, 0:64], lhsT=ones[:], rhs=rows0[:, 2048:2112], start=True, stop=True
             )
+            for u in range(2):
+                rows = slice(64 * u, 64 * u + 64)
+                nc.vector.tensor_copy(out=w32[rows, :], in_=heads[rows, u:8:2])
+                nc.vector.tensor_copy(out=b32[rows, :], in_=heads[rows, 16 + u : 24 : 2])
+                nc.vector.tensor_scalar(
+                    out=dclip[rows, :],
+                    in0=heads[rows, 32 + u : 40 : 2],
+                    scalar1=0.9,
+                    scalar2=1.0,
+                    op0=ALU.max,
+                    op1=ALU.min,
+                )
             nc.scalar.sqrt(droot[:], dclip[:])
             nc.scalar.sqrt(decay[:], droot[:])
             for G in range(4):
@@ -165,6 +171,16 @@ def tile_mixedrepeatheads_kernel(
                 )
             nc.vector.tensor_mul(coef[:, 0:2], w32[:, 0:2], decay[:, 0:2])
             nc.vector.tensor_copy(out=coef[:, 2:4], in_=decay[:, 2:4])
+            for nb in range(4):
+                spread = psum.tile([P, 512], F32, tag="bank")
+                nc.tensor.matmul(
+                    out=spread[:],
+                    lhsT=ones[:],
+                    rhs=rows0[:, nb * 512 : nb * 512 + 512],
+                    start=True,
+                    stop=True,
+                )
+                copy_on(nb % 2, bo[:, nb * 512 : nb * 512 + 512], spread[:])
 
         xc = const.tile([P, 4, 512], U32, align_bytes=64)
         xs = const.tile([P, 4, 512], U8, align_bytes=64)

@@ -15,7 +15,7 @@ P = 128
 FLOPS = 2 * 512 * 2048 * 2048 * 2
 
 RAW_BUFS = 8
-WOUT_V_COLS = (160, 160, 160, 160)
+WOUT_V_COLS = (128, 128, 112, 96)
 
 
 def tile_mixedrepeatheads_kernel(

@@ -62,16 +62,13 @@ def tile_mixedrepeatheads_kernel(
                 if a >= 2:
                     nc.sync.dma_start(out=t[:].rearrange("p (g e) -> p g e", g=4), in_=wp_view(a))
                 elif a == 1:
-                    for g0, g1 in ((0, 1), (1, 4)):
+                    for g in range(4):
                         for h in range(2):
                             nc.sync.dma_start(
-                                out=tiles[("wp", h, 0)][:, g0 * 1024 : g1 * 1024].rearrange(
-                                    "p (g e) -> p g e", e=1024
-                                ),
-                                in_=wp_view(h)[:, g0:g1, :],
+                                out=tiles[("wp", h, 0)][:, g * 1024 : g * 1024 + 1024],
+                                in_=wp_view(h)[:, g, :],
                             )
-                        if g0 == 0:
-                            row_loads()
+                        row_load(g)
             elif kind == "wo":
                 t = rawp.tile([P, 4096], BF16, tag="raw")
                 nc.sync.dma_start(
@@ -110,7 +107,7 @@ def tile_mixedrepeatheads_kernel(
         nc.vector.memset(warm[:], 1.0)
         nc.scalar.sqrt(warm[:], warm[:])
 
-        rows0 = const.tile([P, 2112], BF16)
+        rows0 = const.tile([P, 2624], BF16)
         ones = const.tile([P, P], BF16)
         nc.vector.memset(rows0[:].bitcast(F32), 0.0)
         nc.vector.memset(ones[:], 1.0)
@@ -118,18 +115,20 @@ def tile_mixedrepeatheads_kernel(
         ident = const.tile([P, P], F32)
         masks.make_identity(nc, ident[:])
 
-        bp = const.tile([P, 4, 4], BF16)
-        nc.sync.dma_start(
-            out=bp[:],
-            in_=b_proj.rearrange("h c -> (h c)").rearrange("(g p t) -> p g t", p=P, t=4),
-        )
 
-        def row_loads():
+        def row_load(i):
             with nc.allow_non_contiguous_dma(reason="a few per-head scalars"):
-                nc.sync.dma_start(out=rows0[0:1, 2048:2056], in_=w_mix[:, index].unsqueeze(0))
-                nc.sync.dma_start(out=rows0[0:1, 2064:2072], in_=b_mix[:, index].unsqueeze(0))
-                nc.sync.dma_start(out=rows0[0:1, 2080:2088], in_=decay_values.unsqueeze(0))
-            nc.sync.dma_start(out=rows0[0:1, 0:2048], in_=b_out.unsqueeze(0))
+                if i == 0:
+                    nc.sync.dma_start(out=rows0[0:1, 0:2048], in_=b_out.unsqueeze(0))
+                elif i == 1:
+                    nc.sync.dma_start(out=rows0[0:1, 2048:2056], in_=w_mix[:, index].unsqueeze(0))
+                elif i == 2:
+                    nc.sync.dma_start(out=rows0[0:1, 2064:2072], in_=b_mix[:, index].unsqueeze(0))
+                else:
+                    nc.sync.dma_start(out=rows0[0:1, 2080:2088], in_=decay_values.unsqueeze(0))
+                    nc.sync.dma_start(
+                        out=rows0[0:4, 2112:2624], in_=b_proj.rearrange("(g u) c -> g (u c)", u=2)
+                    )
 
         fetch(RAW_BUFS)
 
@@ -146,6 +145,11 @@ def tile_mixedrepeatheads_kernel(
             nc.tensor.matmul(
                 out=heads[:, 0:64], lhsT=ones[:], rhs=rows0[:, 2048:2112], start=True, stop=True
             )
+            bpw = rows0[:].bitcast(F32)
+            for u2 in range(2):
+                nc.tensor.transpose(
+                    heads[:, 128 + u2 * 128 : 256 + u2 * 128], bpw[:, 1056 + u2 : 1312 : 2], ident[:]
+                )
             for u in range(2):
                 rows = slice(64 * u, 64 * u + 64)
                 nc.vector.tensor_copy(out=w32[rows, :], in_=heads[rows, u:8:2])
@@ -160,10 +164,11 @@ def tile_mixedrepeatheads_kernel(
                 )
             nc.scalar.sqrt(droot[:], dclip[:])
             nc.scalar.sqrt(decay[:], droot[:])
+            bpt = heads[:, 128:384].bitcast(BF16).rearrange("m (u r e) -> m u r e", u=2, e=2)
             for G in range(4):
                 nc.vector.tensor_scalar(
-                    out=bias[:, G, :],
-                    in0=bp[:, G, :],
+                    out=bias[:, G, :].rearrange("m (u e) -> m u e", u=2),
+                    in0=bpt[:, :, G, :],
                     scalar1=w32[:, G : G + 1],
                     scalar2=b32[:, G : G + 1],
                     op0=ALU.mult,
@@ -381,6 +386,8 @@ def tile_mixedrepeatheads_kernel(
         c_scale(0)
         for G in range(1, 4):
             wp_regroup(G, 0)
+            if G >= 2:
+                h_quant(G - 2)
             wp_regroup(G, 1)
             wp_quant(G, 0)
             m1(G - 1, 0)
@@ -399,7 +406,6 @@ def tile_mixedrepeatheads_kernel(
             mix(G - 1, 2)
             m1(G - 1, 3)
             mix(G - 1, 3)
-            h_quant(G - 1)
             c_scale(G)
 
         def behind(nb, i):
@@ -415,6 +421,8 @@ def tile_mixedrepeatheads_kernel(
 
         for nb in range(4):
             wo_regroup(nb, 0)
+            if nb == 0:
+                h_quant(2)
             wo_regroup(nb, 1)
             wo_quant(nb, 0)
             if nb > 0:

@@ -15,7 +15,8 @@ P = 128
 FLOPS = 2 * 512 * 2048 * 2048 * 2
 
 RAW_BUFS = 8
-WOUT_V_COLS = (128, 128, 112, 96)
+WOUT_G_COLS = 128
+WOUT_V_COLS = (32, 32, 32, 32)
 
 
 def tile_mixedrepeatheads_kernel(
@@ -318,8 +319,16 @@ def tile_mixedrepeatheads_kernel(
             wr = tiles[("wo", nb // 2, G)][:].rearrange("p (j n) -> p j n", j=4)
             off = (nb % 2) * 512
             dst = grp_tile(("og", nb, G))[:].rearrange("p (n j) -> p n j", j=4)
-            cut = WOUT_V_COLS[nb]
-            for lo, hi, eng in ((0, cut, 0), (cut, 512, 1)):
+            nc.gpsimd.tensor_scalar(
+                out=dst[:, 0:WOUT_G_COLS, :],
+                in0=wr[:, :, off : off + WOUT_G_COLS].rearrange("p j n -> p n j"),
+                scalar1=1.0,
+                scalar2=0.0,
+                op0=ALU.mult,
+                op1=ALU.add,
+            )
+            cut = WOUT_G_COLS + WOUT_V_COLS[nb]
+            for lo, hi, eng in ((WOUT_G_COLS, cut, 0), (cut, 512, 1)):
                 copy_on(
                     eng,
                     dst[:, lo:hi, :].rearrange("p (c i) j -> p c j i", i=4),

@@ -15,8 +15,7 @@ P = 128
 FLOPS = 2 * 512 * 2048 * 2048 * 2
 
 RAW_BUFS = 8
-WOUT_G_COLS = 128
-WOUT_V_COLS = (32, 32, 32, 32)
+WOUT_V_COLS = ((0, 256, 0, 256), (0, 256, 0, 256), (0, 224, 0, 224), (0, 192, 0, 192))
 
 
 def tile_mixedrepeatheads_kernel(
@@ -319,16 +318,10 @@ def tile_mixedrepeatheads_kernel(
             wr = tiles[("wo", nb // 2, G)][:].rearrange("p (j n) -> p j n", j=4)
             off = (nb % 2) * 512
             dst = grp_tile(("og", nb, G))[:].rearrange("p (n j) -> p n j", j=4)
-            nc.gpsimd.tensor_scalar(
-                out=dst[:, 0:WOUT_G_COLS, :],
-                in0=wr[:, :, off : off + WOUT_G_COLS].rearrange("p j n -> p n j"),
-                scalar1=1.0,
-                scalar2=0.0,
-                op0=ALU.mult,
-                op1=ALU.add,
-            )
-            cut = WOUT_G_COLS + WOUT_V_COLS[nb]
-            for lo, hi, eng in ((WOUT_G_COLS, cut, 0), (cut, 512, 1)):
+            cut = WOUT_V_COLS[nb][G]
+            for lo, hi, eng in ((0, cut, 0), (cut, 512, 1)):
+                if lo == hi:
+                    continue
                 copy_on(
                     eng,
                     dst[:, lo:hi, :].rearrange("p (c i) j -> p c j i", i=4),

@@ -15,7 +15,7 @@ P = 128
 FLOPS = 2 * 512 * 2048 * 2048 * 2
 
 RAW_BUFS = 8
-WOUT_V_COLS = ((0, 256, 0, 256), (0, 256, 0, 256), (0, 224, 0, 224), (0, 192, 0, 192))
+WOUT_V_COLS = (128, 128, 112, 96)
 
 
 def tile_mixedrepeatheads_kernel(
@@ -23,7 +23,6 @@ def tile_mixedrepeatheads_kernel(
 ):
     nc = tc.nc
     with ExitStack() as ctx:
-        ctx.enter_context(tc.manual_schedule())
         const = ctx.enter_context(tc.tile_pool(name="const", bufs=1))
         rawp = ctx.enter_context(tc.tile_pool(name="rawp", bufs=RAW_BUFS))
         grpp = ctx.enter_context(tc.tile_pool(name="grpp", bufs=6))
@@ -318,10 +317,8 @@ def tile_mixedrepeatheads_kernel(
             wr = tiles[("wo", nb // 2, G)][:].rearrange("p (j n) -> p j n", j=4)
             off = (nb % 2) * 512
             dst = grp_tile(("og", nb, G))[:].rearrange("p (n j) -> p n j", j=4)
-            cut = WOUT_V_COLS[nb][G]
+            cut = WOUT_V_COLS[nb]
             for lo, hi, eng in ((0, cut, 0), (cut, 512, 1)):
-                if lo == hi:
-                    continue
                 copy_on(
                     eng,
                     dst[:, lo:hi, :].rearrange("p (c i) j -> p c j i", i=4),

@@ -14,8 +14,19 @@ ACT = mybir.ActivationFunctionType
 P = 128
 FLOPS = 2 * 512 * 2048 * 2048 * 2
 
+VECTOR = 0
+SCALAR = 1
+
 RAW_BUFS = 8
-WOUT_V_COLS = (128, 128, 112, 96)
+
+WOUT_VECTOR_COLS = (128, 128, 112, 96)
+
+COL_W = 2048
+COL_B = 2064
+COL_DECAY = 2080
+COL_HEADS_END = 2112
+COL_B_PROJ = 2112
+SMALL_COLS = 2624
 
 
 def tile_mixedrepeatheads_kernel(
@@ -23,182 +34,199 @@ def tile_mixedrepeatheads_kernel(
 ):
     nc = tc.nc
     with ExitStack() as ctx:
+        ctx.enter_context(tc.manual_schedule())
         const = ctx.enter_context(tc.tile_pool(name="const", bufs=1))
-        rawp = ctx.enter_context(tc.tile_pool(name="rawp", bufs=RAW_BUFS))
-        grpp = ctx.enter_context(tc.tile_pool(name="grpp", bufs=6))
-        cachep = ctx.enter_context(tc.tile_pool(name="cachep", bufs=4))
-        wqp = ctx.enter_context(tc.tile_pool(name="wqp", bufs=2))
-        ctpp = ctx.enter_context(tc.tile_pool(name="ctpp", bufs=2))
-        outp = ctx.enter_context(tc.tile_pool(name="outp", bufs=2))
+        raw_pool = ctx.enter_context(tc.tile_pool(name="raw", bufs=RAW_BUFS))
+        grouped_pool = ctx.enter_context(tc.tile_pool(name="grouped", bufs=6))
+        caches_pool = ctx.enter_context(tc.tile_pool(name="caches", bufs=4))
+        wproj_pool = ctx.enter_context(tc.tile_pool(name="wproj", bufs=2))
+        addend_pool = ctx.enter_context(tc.tile_pool(name="addend", bufs=2))
+        result_pool = ctx.enter_context(tc.tile_pool(name="result", bufs=2))
         psum = ctx.enter_context(tc.psum_pool(name="psum", bufs=8))
 
-        bo = const.tile([P, 2048], BF16)
-        plan = [("wp", 0, 0), ("wp", 1, 0), ("x", 0, 0), ("x", 1, 0), ("c", 0, 0)]
-        for G in range(1, 4):
-            plan.append(("wp", 2 * G, 0))
-            plan.append(("wp", 2 * G + 1, 0))
-            plan.append(("c", G, 0))
-        for half in range(2):
-            for G in range(4):
-                plan.append(("wo", half, G))
-        state = {"pos": 0, "raw": 0, "done": 0}
-        tiles = {}
-        xview = x.rearrange("(p r) k -> p r k", r=4)
+        b_out_all = const.tile([P, 2048], BF16)
 
-        def wp_view(h):
-            return W_proj[h].rearrange("(g p j) c -> p g (j c)", g=4, p=P, j=4)
+        plan = [("wp", 0, 0), ("wp", 1, 0), ("x", 0, 0), ("x", 1, 0), ("c", 0, 0)]
+        for pair in range(1, 4):
+            plan.append(("wp", 2 * pair, 0))
+            plan.append(("wp", 2 * pair + 1, 0))
+            plan.append(("c", pair, 0))
+        for col_half in range(2):
+            for pair in range(4):
+                plan.append(("wo", col_half, pair))
+        progress = {"issued": 0, "raw_issued": 0, "raw_read": 0}
+        loaded = {}
+        x_rows = x.rearrange("(p s) k -> p s k", s=4)
+
+        def wproj_rows(head):
+            return W_proj[head].rearrange("(g p j) c -> p g (j c)", g=4, p=P, j=4)
 
         def issue(kind, a, b):
             if kind == "x":
-                t = rawp.tile([P, 4096], BF16, tag="raw")
+                raw = raw_pool.tile([P, 4096], BF16, tag="raw")
                 nc.sync.dma_start(
-                    out=t[:].rearrange("p (r k) -> p r k", r=2), in_=xview[:, 2 * a : 2 * a + 2, :]
+                    out=raw[:].rearrange("p (s k) -> p s k", s=2), in_=x_rows[:, 2 * a : 2 * a + 2, :]
                 )
-                tiles[(kind, a, b)] = t
+                loaded[(kind, a, b)] = raw
             elif kind == "wp":
-                t = rawp.tile([P, 4096], BF16, tag="raw")
-                tiles[(kind, a, b)] = t
+                raw = raw_pool.tile([P, 4096], BF16, tag="raw")
+                loaded[(kind, a, b)] = raw
                 if a >= 2:
-                    nc.sync.dma_start(out=t[:].rearrange("p (g e) -> p g e", g=4), in_=wp_view(a))
+                    nc.sync.dma_start(
+                        out=raw[:].rearrange("p (g y) -> p g y", g=4), in_=wproj_rows(a)
+                    )
                 elif a == 1:
                     for g in range(4):
-                        for h in range(2):
+                        for head in range(2):
                             nc.sync.dma_start(
-                                out=tiles[("wp", h, 0)][:, g * 1024 : g * 1024 + 1024],
-                                in_=wp_view(h)[:, g, :],
+                                out=loaded[("wp", head, 0)][:, g * 1024 : g * 1024 + 1024],
+                                in_=wproj_rows(head)[:, g, :],
                             )
-                        row_load(g)
+                        load_small_rows(g)
             elif kind == "wo":
-                t = rawp.tile([P, 4096], BF16, tag="raw")
+                raw = raw_pool.tile([P, 4096], BF16, tag="raw")
                 nc.sync.dma_start(
-                    out=t[:].rearrange("p (j n) -> p j n", j=4),
+                    out=raw[:].rearrange("p (j n) -> p j n", j=4),
                     in_=W_out[512 * b : 512 * b + 512, 1024 * a : 1024 * a + 1024].rearrange(
                         "(p j) n -> p j n", j=4
                     ),
                 )
-                tiles[(kind, a, b)] = t
+                loaded[(kind, a, b)] = raw
             else:
-                t = cachep.tile([P, 2048], BF16, tag="craw")
-                tv = t[:].rearrange("p (r c) -> p r c", r=4)
-                for u in range(2):
+                raw = caches_pool.tile([P, 2048], BF16, tag="caches")
+                by_group = raw[:].rearrange("p (s c) -> p s c", s=4)
+                for head in range(2):
                     nc.sync.dma_start(
-                        out=tv[:, :, 256 * u : 256 * u + 256],
-                        in_=caches[2 * a + u].rearrange("(p r) c -> p r c", r=4),
+                        out=by_group[:, :, 256 * head : 256 * head + 256],
+                        in_=caches[2 * a + head].rearrange("(p s) c -> p s c", s=4),
                     )
-                tiles[(kind, a, b)] = t
+                loaded[(kind, a, b)] = raw
 
-        def fetch(raw_count):
-            while state["pos"] < len(plan):
-                kind, a, b = plan[state["pos"]]
-                is_raw = kind in ("x", "wp", "wo")
-                if is_raw and state["raw"] >= raw_count:
+        def issue_until(raw_tiles):
+            while progress["issued"] < len(plan):
+                kind, a, b = plan[progress["issued"]]
+                takes_raw_tile = kind in ("x", "wp", "wo")
+                if takes_raw_tile and progress["raw_issued"] >= raw_tiles:
                     break
                 issue(kind, a, b)
-                state["pos"] += 1
-                if is_raw:
-                    state["raw"] += 1
+                progress["issued"] += 1
+                if takes_raw_tile:
+                    progress["raw_issued"] += 1
 
-        def retire(count):
-            state["done"] += count
-            fetch(state["done"] + RAW_BUFS)
+        def raw_tiles_read(count):
+            progress["raw_read"] += count
+            issue_until(progress["raw_read"] + RAW_BUFS)
 
-        warm = const.tile([P, 1], F32)
-        nc.vector.memset(warm[:], 1.0)
-        nc.scalar.sqrt(warm[:], warm[:])
+        scratch = const.tile([P, 1], F32)
+        nc.vector.memset(scratch[:], 1.0)
+        nc.scalar.sqrt(scratch[:], scratch[:])
 
-        rows0 = const.tile([P, 2624], BF16)
+        small = const.tile([P, SMALL_COLS], BF16)
         ones = const.tile([P, P], BF16)
-        nc.vector.memset(rows0[:].bitcast(F32), 0.0)
+        nc.vector.memset(small[:].bitcast(F32), 0.0)
         nc.vector.memset(ones[:], 1.0)
 
         ident = const.tile([P, P], F32)
         masks.make_identity(nc, ident[:])
 
-
-        def row_load(i):
-            with nc.allow_non_contiguous_dma(reason="a few per-head scalars"):
-                if i == 0:
-                    nc.sync.dma_start(out=rows0[0:1, 0:2048], in_=b_out.unsqueeze(0))
-                elif i == 1:
-                    nc.sync.dma_start(out=rows0[0:1, 2048:2056], in_=w_mix[:, index].unsqueeze(0))
-                elif i == 2:
-                    nc.sync.dma_start(out=rows0[0:1, 2064:2072], in_=b_mix[:, index].unsqueeze(0))
-                else:
-                    nc.sync.dma_start(out=rows0[0:1, 2080:2088], in_=decay_values.unsqueeze(0))
+        def load_small_rows(step):
+            with nc.allow_non_contiguous_dma(reason="eight scalars, one of each head"):
+                if step == 0:
+                    nc.sync.dma_start(out=small[0:1, 0:2048], in_=b_out.unsqueeze(0))
+                elif step == 1:
                     nc.sync.dma_start(
-                        out=rows0[0:4, 2112:2624], in_=b_proj.rearrange("(g u) c -> g (u c)", u=2)
+                        out=small[0:1, COL_W : COL_W + 8], in_=w_mix[:, index].unsqueeze(0)
+                    )
+                elif step == 2:
+                    nc.sync.dma_start(
+                        out=small[0:1, COL_B : COL_B + 8], in_=b_mix[:, index].unsqueeze(0)
+                    )
+                else:
+                    nc.sync.dma_start(
+                        out=small[0:1, COL_DECAY : COL_DECAY + 8], in_=decay_values.unsqueeze(0)
+                    )
+                    nc.sync.dma_start(
+                        out=small[0:4, COL_B_PROJ:SMALL_COLS],
+                        in_=b_proj.rearrange("(a h) c -> a (h c)", h=2),
                     )
 
-        fetch(RAW_BUFS)
+        issue_until(RAW_BUFS)
 
-        w32 = const.tile([P, 4], F32)
-        b32 = const.tile([P, 4], F32)
-        dclip = const.tile([P, 4], F32)
-        droot = const.tile([P, 4], F32)
+        w_col = const.tile([P, 4], F32)
+        b_col = const.tile([P, 4], F32)
+        clipped = const.tile([P, 4], F32)
+        root = const.tile([P, 4], F32)
         decay = const.tile([P, 4], F32)
         coef = const.tile([P, 4], F32)
         bias = const.tile([P, 4, 4], F32)
 
-        def small_vectors():
-            heads = psum.tile([P, 512], F32, tag="bank")
+        def prepare_small_vectors():
+            spread = psum.tile([P, 512], F32, tag="bank")
+            at_b = COL_B - COL_W
+            at_decay = COL_DECAY - COL_W
             nc.tensor.matmul(
-                out=heads[:, 0:64], lhsT=ones[:], rhs=rows0[:, 2048:2112], start=True, stop=True
+                out=spread[:, 0:64],
+                lhsT=ones[:],
+                rhs=small[:, COL_W:COL_HEADS_END],
+                start=True,
+                stop=True,
             )
-            bpw = rows0[:].bitcast(F32)
-            for u2 in range(2):
+            small_f32 = small[:].bitcast(F32)
+            for v in range(2):
                 nc.tensor.transpose(
-                    heads[:, 128 + u2 * 128 : 256 + u2 * 128], bpw[:, 1056 + u2 : 1312 : 2], ident[:]
+                    spread[:, 128 + v * 128 : 256 + v * 128],
+                    small_f32[:, COL_B_PROJ // 2 + v : SMALL_COLS // 2 : 2],
+                    ident[:],
                 )
-            for u in range(2):
-                rows = slice(64 * u, 64 * u + 64)
-                nc.vector.tensor_copy(out=w32[rows, :], in_=heads[rows, u:8:2])
-                nc.vector.tensor_copy(out=b32[rows, :], in_=heads[rows, 16 + u : 24 : 2])
+            for head in range(2):
+                part = slice(64 * head, 64 * head + 64)
+                nc.vector.tensor_copy(out=w_col[part, :], in_=spread[part, head:8:2])
+                nc.vector.tensor_copy(
+                    out=b_col[part, :], in_=spread[part, at_b + head : at_b + 8 : 2]
+                )
                 nc.vector.tensor_scalar(
-                    out=dclip[rows, :],
-                    in0=heads[rows, 32 + u : 40 : 2],
+                    out=clipped[part, :],
+                    in0=spread[part, at_decay + head : at_decay + 8 : 2],
                     scalar1=0.9,
                     scalar2=1.0,
                     op0=ALU.max,
                     op1=ALU.min,
                 )
-            nc.scalar.sqrt(droot[:], dclip[:])
-            nc.scalar.sqrt(decay[:], droot[:])
-            bpt = heads[:, 128:384].bitcast(BF16).rearrange("m (u r e) -> m u r e", u=2, e=2)
-            for G in range(4):
+            nc.scalar.sqrt(root[:], clipped[:])
+            nc.scalar.sqrt(decay[:], root[:])
+            b_proj_t = spread[:, 128:384].bitcast(BF16).rearrange("m (v r e) -> m v r e", v=2, e=2)
+            for pair in range(4):
                 nc.vector.tensor_scalar(
-                    out=bias[:, G, :].rearrange("m (u e) -> m u e", u=2),
-                    in0=bpt[:, :, G, :],
-                    scalar1=w32[:, G : G + 1],
-                    scalar2=b32[:, G : G + 1],
+                    out=bias[:, pair, :].rearrange("m (v e) -> m v e", v=2),
+                    in0=b_proj_t[:, :, pair, :],
+                    scalar1=w_col[:, pair : pair + 1],
+                    scalar2=b_col[:, pair : pair + 1],
                     op0=ALU.mult,
                     op1=ALU.add,
                 )
-            nc.vector.tensor_mul(coef[:, 0:2], w32[:, 0:2], decay[:, 0:2])
+            nc.vector.tensor_mul(coef[:, 0:2], w_col[:, 0:2], decay[:, 0:2])
             nc.vector.tensor_copy(out=coef[:, 2:4], in_=decay[:, 2:4])
-            for nb in range(4):
-                spread = psum.tile([P, 512], F32, tag="bank")
+            for panel in range(4):
+                cols = slice(panel * 512, panel * 512 + 512)
+                repeated = psum.tile([P, 512], F32, tag="bank")
                 nc.tensor.matmul(
-                    out=spread[:],
-                    lhsT=ones[:],
-                    rhs=rows0[:, nb * 512 : nb * 512 + 512],
-                    start=True,
-                    stop=True,
+                    out=repeated[:], lhsT=ones[:], rhs=small[:, cols], start=True, stop=True
                 )
-                copy_on(nb % 2, bo[:, nb * 512 : nb * 512 + 512], spread[:])
+                copy_on(panel % 2, b_out_all[:, cols], repeated[:])
 
-        xc = const.tile([P, 4, 512], U32, align_bytes=64)
-        xs = const.tile([P, 4, 512], U8, align_bytes=64)
-        hc = const.tile([P, 4, 512], U32, align_bytes=64)
-        hs = const.tile([P, 4, 512], U8, align_bytes=64)
-        woc = const.tile([P, 16, 512], U32, align_bytes=64)
-        wos = const.tile([P, 16, 512], U8, align_bytes=64)
+        x_words = const.tile([P, 4, 512], U32, align_bytes=64)
+        x_scales = const.tile([P, 4, 512], U8, align_bytes=64)
+        hidden_words = const.tile([P, 4, 512], U32, align_bytes=64)
+        hidden_scales = const.tile([P, 4, 512], U8, align_bytes=64)
+        wout_words = const.tile([P, 16, 512], U32, align_bytes=64)
+        wout_scales = const.tile([P, 16, 512], U8, align_bytes=64)
 
         live = {}
 
-        def grp_tile(key):
+        def grouped_tile(key):
             if key not in live:
-                gt = grpp.tile([P, 2048], BF16, tag="grp", align_bytes=64)
-                live[key] = gt
+                grouped = grouped_pool.tile([P, 2048], BF16, tag="grouped", align_bytes=64)
+                live[key] = grouped
             return live[key]
 
         def new_bank(key):
@@ -206,246 +234,244 @@ def tile_mixedrepeatheads_kernel(
             live[key] = bank
             return bank
 
-        def copy_on(eng, dst, src):
-            if eng == 0:
+        def copy_on(engine, dst, src):
+            if engine == VECTOR:
                 nc.vector.tensor_copy(out=dst, in_=src)
             else:
                 nc.scalar.copy(out=dst, in_=src)
 
-        def x_bank(rp, g):
-            xw = tiles[("x", rp, 0)][:].bitcast(F32)
-            bank = new_bank(("xb", rp, g))
+        def transpose_x(x_half, g):
+            x_f32 = loaded[("x", x_half, 0)][:].bitcast(F32)
+            bank = new_bank(("x", x_half, g))
             for u in range(2):
-                for rl in range(2):
-                    base = rl * 1024 + 256 * g
+                for within in range(2):
+                    first = within * 1024 + 256 * g
                     nc.tensor.transpose(
-                        bank[:, u * 256 + rl * 128 : u * 256 + rl * 128 + 128],
-                        xw[:, base + u : base + 256 : 2],
+                        bank[:, u * 256 + within * 128 : u * 256 + within * 128 + 128],
+                        x_f32[:, first + u : first + 256 : 2],
                         ident[:],
                     )
             copy_on(
                 (g + 1) % 2,
-                grp_tile(("xg", g))[:].bitcast(F32).rearrange("q (r u) -> q r u", u=2)[
-                    :, rp * 256 : rp * 256 + 256, :
+                grouped_tile(("x", g))[:].bitcast(F32).rearrange("q (r u) -> q r u", u=2)[
+                    :, x_half * 256 : x_half * 256 + 256, :
                 ],
                 bank[:].rearrange("q (u r) -> q r u", u=2),
             )
 
-        def x_quant(g):
+        def quantise_x(g):
             nc.vector.quantize_mx(
-                out=xc[:, g, :].bitcast(FP8X4), scales=xs[:, g, :], in_=grp_tile(("xg", g))[:]
+                out=x_words[:, g, :].bitcast(FP8X4),
+                scales=x_scales[:, g, :],
+                in_=grouped_tile(("x", g))[:],
             )
 
-        def wp_regroup(G, g):
-            dst = grp_tile(("wg", G, g))[:].rearrange("p (t m j) -> p t m j", t=4, m=P, j=4)
-            for u in range(2):
-                src = tiles[("wp", 2 * G + u, 0)][:, g * 1024 : g * 1024 + 1024].rearrange(
+        def regroup_wproj(pair, g):
+            dst = grouped_tile(("wproj", pair, g))[:].rearrange("p (t m j) -> p t m j", t=4, m=P, j=4)
+            for head in range(2):
+                src = loaded[("wp", 2 * pair + head, 0)][:, g * 1024 : g * 1024 + 1024].rearrange(
                     "p (j m t) -> p m j t", j=4, m=64, t=4
                 )
-                dstu = dst[:, :, 64 * u : 64 * u + 64, :].rearrange("p t m j -> p m j t")
-                copy_on((g + u) % 2, dstu, src)
-
-        def wp_quant(G, g):
-            if ("wpc", G) not in live:
-                wpc = wqp.tile([P, 4, 512], U32, tag="wpc", align_bytes=64)
-                wps = wqp.tile([P, 4, 512], U8, tag="wps", align_bytes=64)
-                live[("wpc", G)] = wpc
-                live[("wps", G)] = wps
-            nc.vector.quantize_mx(
-                out=live[("wpc", G)][:, g, :].bitcast(FP8X4),
-                scales=live[("wps", G)][:, g, :],
-                in_=grp_tile(("wg", G, g))[:],
-            )
-
-        def c_transpose(G, u2):
-            cw = tiles[("c", G, 0)][:].bitcast(F32).rearrange("p (r w) -> p r w", r=4)
-            bank = new_bank(("cb", G, u2))
-            for rr in range(4):
-                nc.tensor.transpose(
-                    bank[:, rr * 128 : rr * 128 + 128], cw[:, rr, u2 : 256 : 2], ident[:]
+                copy_on(
+                    (g + head) % 2,
+                    dst[:, :, 64 * head : 64 * head + 64, :].rearrange("p t m j -> p m j t"),
+                    src,
                 )
 
-        def c_scale(G):
-            ctp = ctpp.tile([P, 4, 512], F32, tag="ctp")
-            live[("ctp", G)] = ctp
-            for u2 in range(2):
-                bview = live[("cb", G, u2)][:].bitcast(BF16).rearrange("m (r e) -> m r e", e=2)
+        def quantise_wproj(pair, g):
+            if ("wproj words", pair) not in live:
+                wproj_words = wproj_pool.tile([P, 4, 512], U32, tag="words", align_bytes=64)
+                wproj_scales = wproj_pool.tile([P, 4, 512], U8, tag="scales", align_bytes=64)
+                live[("wproj words", pair)] = wproj_words
+                live[("wproj scales", pair)] = wproj_scales
+            nc.vector.quantize_mx(
+                out=live[("wproj words", pair)][:, g, :].bitcast(FP8X4),
+                scales=live[("wproj scales", pair)][:, g, :],
+                in_=grouped_tile(("wproj", pair, g))[:],
+            )
+
+        def transpose_caches(pair, v):
+            caches_f32 = loaded[("c", pair, 0)][:].bitcast(F32).rearrange("p (s w) -> p s w", s=4)
+            bank = new_bank(("caches", pair, v))
+            for s in range(4):
+                nc.tensor.transpose(
+                    bank[:, s * 128 : s * 128 + 128], caches_f32[:, s, v : 256 : 2], ident[:]
+                )
+
+        def scale_caches(pair):
+            addend = addend_pool.tile([P, 4, 512], F32, tag="addend")
+            live[("addend", pair)] = addend
+            for v in range(2):
+                halves = live[("caches", pair, v)][:].bitcast(BF16).rearrange("m (r e) -> m r e", e=2)
                 for e in range(2):
-                    t = 2 * u2 + e
+                    t = 2 * v + e
                     nc.scalar.activation(
-                        out=ctp[:, t, :],
-                        in_=bview[:, :, e],
+                        out=addend[:, t, :],
+                        in_=halves[:, :, e],
                         func=ACT.Identity,
-                        bias=bias[:, G, t : t + 1],
-                        scale=coef[:, G : G + 1],
+                        bias=bias[:, pair, t : t + 1],
+                        scale=coef[:, pair : pair + 1],
                     )
 
-        def m1(G, rr):
-            bank = new_bank(("mb", G, rr))
-            wpc = live[("wpc", G)]
-            wps = live[("wps", G)]
+        def project(pair, s):
+            bank = new_bank(("proj", pair, s))
+            w_words = live[("wproj words", pair)]
+            w_scales = live[("wproj scales", pair)]
             for t in range(4):
                 for g in range(4):
                     nc.tensor.matmul_mx(
                         out=bank[:, t * 128 : t * 128 + 128],
-                        lhsT=wpc[:, g, t * 128 : t * 128 + 128].bitcast(FP8X4),
-                        lhsT_scale=wps[:, g, t * 128 : t * 128 + 128],
-                        rhs=xc[:, g, rr * 128 : rr * 128 + 128].bitcast(FP8X4),
-                        rhs_scale=xs[:, g, rr * 128 : rr * 128 + 128],
+                        lhsT=w_words[:, g, t * 128 : t * 128 + 128].bitcast(FP8X4),
+                        lhsT_scale=w_scales[:, g, t * 128 : t * 128 + 128],
+                        rhs=x_words[:, g, s * 128 : s * 128 + 128].bitcast(FP8X4),
+                        rhs_scale=x_scales[:, g, s * 128 : s * 128 + 128],
                         start=(g == 0),
                         stop=(g == 3),
                     )
 
-        def mix(G, rr):
+        def mix(pair, s):
             nc.vector.scalar_tensor_tensor(
-                out=grp_tile(("hg", G))[:, rr * 512 : rr * 512 + 512].rearrange(
+                out=grouped_tile(("hidden", pair))[:, s * 512 : s * 512 + 512].rearrange(
                     "m (r t) -> m r t", t=4
                 ),
-                in0=live[("mb", G, rr)][:].rearrange("m (t r) -> m r t", t=4),
-                scalar=w32[:, G : G + 1],
-                in1=live[("ctp", G)][:, :, rr * 128 : rr * 128 + 128].rearrange("m t r -> m r t"),
+                in0=live[("proj", pair, s)][:].rearrange("m (t r) -> m r t", t=4),
+                scalar=w_col[:, pair : pair + 1],
+                in1=live[("addend", pair)][:, :, s * 128 : s * 128 + 128].rearrange("m t r -> m r t"),
                 op0=ALU.mult,
                 op1=ALU.add,
             )
 
-        def h_quant(G):
+        def quantise_hidden(pair):
             nc.vector.quantize_mx(
-                out=hc[:, G, :].bitcast(FP8X4), scales=hs[:, G, :], in_=grp_tile(("hg", G))[:]
+                out=hidden_words[:, pair, :].bitcast(FP8X4),
+                scales=hidden_scales[:, pair, :],
+                in_=grouped_tile(("hidden", pair))[:],
             )
 
-        def wo_regroup(nb, G):
-            wr = tiles[("wo", nb // 2, G)][:].rearrange("p (j n) -> p j n", j=4)
-            off = (nb % 2) * 512
-            dst = grp_tile(("og", nb, G))[:].rearrange("p (n j) -> p n j", j=4)
-            cut = WOUT_V_COLS[nb]
-            for lo, hi, eng in ((0, cut, 0), (cut, 512, 1)):
+        def regroup_wout(panel, pair):
+            rows = loaded[("wo", panel // 2, pair)][:].rearrange("p (j n) -> p j n", j=4)
+            first = (panel % 2) * 512
+            dst = grouped_tile(("wout", panel, pair))[:].rearrange("p (n j) -> p n j", j=4)
+            cut = WOUT_VECTOR_COLS[panel]
+            for lo, hi, engine in ((0, cut, VECTOR), (cut, 512, SCALAR)):
                 copy_on(
-                    eng,
-                    dst[:, lo:hi, :].rearrange("p (c i) j -> p c j i", i=4),
-                    wr[:, :, off + lo : off + hi].rearrange("p j (c i) -> p c j i", i=4),
+                    engine,
+                    dst[:, lo:hi, :].rearrange("p (f i) j -> p f j i", i=4),
+                    rows[:, :, first + lo : first + hi].rearrange("p j (f i) -> p f j i", i=4),
                 )
 
-        def wo_quant(nb, G):
+        def quantise_wout(panel, pair):
             nc.vector.quantize_mx(
-                out=woc[:, nb * 4 + G, :].bitcast(FP8X4),
-                scales=wos[:, nb * 4 + G, :],
-                in_=grp_tile(("og", nb, G))[:],
+                out=wout_words[:, panel * 4 + pair, :].bitcast(FP8X4),
+                scales=wout_scales[:, panel * 4 + pair, :],
+                in_=grouped_tile(("wout", panel, pair))[:],
             )
 
-        def m2(nb, G):
-            for rr in range(4):
-                if G == 0:
-                    new_bank(("ob", nb, rr))
+        def multiply_out(panel, pair):
+            for s in range(4):
+                if pair == 0:
+                    new_bank(("out", panel, s))
                 nc.tensor.matmul_mx(
-                    out=live[("ob", nb, rr)][:],
-                    lhsT=hc[:, G, rr * 128 : rr * 128 + 128].bitcast(FP8X4),
-                    lhsT_scale=hs[:, G, rr * 128 : rr * 128 + 128],
-                    rhs=woc[:, nb * 4 + G, :].bitcast(FP8X4),
-                    rhs_scale=wos[:, nb * 4 + G, :],
-                    start=(G == 0),
-                    stop=(G == 3),
+                    out=live[("out", panel, s)][:],
+                    lhsT=hidden_words[:, pair, s * 128 : s * 128 + 128].bitcast(FP8X4),
+                    lhsT_scale=hidden_scales[:, pair, s * 128 : s * 128 + 128],
+                    rhs=wout_words[:, panel * 4 + pair, :].bitcast(FP8X4),
+                    rhs_scale=wout_scales[:, panel * 4 + pair, :],
+                    start=(pair == 0),
+                    stop=(pair == 3),
                 )
 
-        oview = out.rearrange("(p r) n -> p r n", r=4)
+        out_rows = out.rearrange("(p s) n -> p s n", s=4)
 
-        def add_bias(nb, rr):
-            if ("ost", nb) not in live:
-                ost = outp.tile([P, 4, 512], F32, tag="ost")
-                live[("ost", nb)] = ost
+        def add_b_out(panel, s):
+            if ("result", panel) not in live:
+                result = result_pool.tile([P, 4, 512], F32, tag="result")
+                live[("result", panel)] = result
             nc.vector.tensor_tensor(
-                out=live[("ost", nb)][:, rr, :],
-                in0=live[("ob", nb, rr)][:],
-                in1=bo[:, nb * 512 : nb * 512 + 512],
+                out=live[("result", panel)][:, s, :],
+                in0=live[("out", panel, s)][:],
+                in1=b_out_all[:, panel * 512 : panel * 512 + 512],
                 op=ALU.add,
             )
 
-        def store(nb, r0, r1):
+        def store(panel, s0, s1):
             nc.sync.dma_start(
-                out=oview[:, r0:r1, nb * 512 : nb * 512 + 512], in_=live[("ost", nb)][:, r0:r1, :]
+                out=out_rows[:, s0:s1, panel * 512 : panel * 512 + 512],
+                in_=live[("result", panel)][:, s0:s1, :],
             )
 
-        wp_regroup(0, 0)
-        wp_regroup(0, 1)
-        wp_quant(0, 0)
-        wp_regroup(0, 2)
-        wp_quant(0, 1)
-        wp_regroup(0, 3)
-        wp_quant(0, 2)
-        wp_quant(0, 3)
-        retire(2)
-        small_vectors()
-        for rp in range(2):
+
+        regroup_wproj(0, 0)
+        for g in range(1, 4):
+            regroup_wproj(0, g)
+            quantise_wproj(0, g - 1)
+        quantise_wproj(0, 3)
+        raw_tiles_read(2)
+        prepare_small_vectors()
+        for x_half in range(2):
             for g in range(4):
-                x_bank(rp, g)
-            retire(1)
+                transpose_x(x_half, g)
+            raw_tiles_read(1)
         for g in range(4):
-            x_quant(g)
-        c_transpose(0, 0)
-        c_transpose(0, 1)
-        c_scale(0)
-        for G in range(1, 4):
-            wp_regroup(G, 0)
-            if G >= 2:
-                h_quant(G - 2)
-            wp_regroup(G, 1)
-            wp_quant(G, 0)
-            m1(G - 1, 0)
-            wp_regroup(G, 2)
-            wp_quant(G, 1)
-            mix(G - 1, 0)
-            m1(G - 1, 1)
-            wp_regroup(G, 3)
-            retire(2)
-            wp_quant(G, 2)
-            mix(G - 1, 1)
-            c_transpose(G, 0)
-            c_transpose(G, 1)
-            m1(G - 1, 2)
-            wp_quant(G, 3)
-            mix(G - 1, 2)
-            m1(G - 1, 3)
-            mix(G - 1, 3)
-            c_scale(G)
+            quantise_x(g)
+        transpose_caches(0, 0)
+        transpose_caches(0, 1)
+        scale_caches(0)
 
-        def behind(nb, i):
-            if nb == 0:
-                m1(3, i)
-                mix(3, i)
-                if i == 3:
-                    h_quant(3)
-            else:
-                add_bias(nb - 1, i)
-                if i % 2 == 1:
-                    store(nb - 1, i - 1, i + 1)
+        for pair in range(1, 4):
+            before = pair - 1
+            regroup_wproj(pair, 0)
+            if pair >= 2:
+                quantise_hidden(pair - 2)
+            regroup_wproj(pair, 1)
+            quantise_wproj(pair, 0)
+            project(before, 0)
+            regroup_wproj(pair, 2)
+            quantise_wproj(pair, 1)
+            mix(before, 0)
+            project(before, 1)
+            regroup_wproj(pair, 3)
+            raw_tiles_read(2)
+            quantise_wproj(pair, 2)
+            mix(before, 1)
+            transpose_caches(pair, 0)
+            transpose_caches(pair, 1)
+            project(before, 2)
+            quantise_wproj(pair, 3)
+            mix(before, 2)
+            project(before, 3)
+            mix(before, 3)
+            scale_caches(pair)
 
-        for nb in range(4):
-            wo_regroup(nb, 0)
-            if nb == 0:
-                h_quant(2)
-            wo_regroup(nb, 1)
-            wo_quant(nb, 0)
-            if nb > 0:
-                m2(nb, 0)
-            behind(nb, 0)
-            wo_regroup(nb, 2)
-            wo_quant(nb, 1)
-            if nb > 0:
-                m2(nb, 1)
-            behind(nb, 1)
-            wo_regroup(nb, 3)
-            wo_quant(nb, 2)
-            if nb > 0:
-                m2(nb, 2)
-            behind(nb, 2)
-            wo_quant(nb, 3)
-            behind(nb, 3)
-            if nb == 0:
-                for G in range(4):
-                    m2(0, G)
+        def beside(panel, s):
+            if panel == 0:
+                project(3, s)
+                mix(3, s)
+                if s == 3:
+                    quantise_hidden(3)
             else:
-                m2(nb, 3)
-            if nb % 2 == 1:
-                retire(4)
-        for rr in range(4):
-            add_bias(3, rr)
-            store(3, rr, rr + 1)
+                add_b_out(panel - 1, s)
+                if s % 2 == 1:
+                    store(panel - 1, s - 1, s + 1)
+
+        for panel in range(4):
+            regroup_wout(panel, 0)
+            if panel == 0:
+                quantise_hidden(2)
+            for pair in range(4):
+                if pair < 3:
+                    regroup_wout(panel, pair + 1)
+                quantise_wout(panel, pair)
+                if pair < 3:
+                    if panel > 0:
+                        multiply_out(panel, pair)
+                    beside(panel, pair)
+            beside(panel, 3)
+            if panel == 0:
+                for pair in range(4):
+                    multiply_out(0, pair)
+            else:
+                multiply_out(panel, 3)
+        for s in range(4):
+            add_b_out(3, s)
+            store(3, s, s + 1)

@@ -46,10 +46,12 @@ def tile_mixedrepeatheads_kernel(
 
         b_out_all = const.tile([P, 2048], BF16)
 
-        plan = [("wp", 0, 0), ("wp", 1, 0), ("x", 0, 0), ("x", 1, 0), ("c", 0, 0)]
+        plan = [("wp", 0, 0), ("wp", 0, 1), ("x", 0, 0), ("x", 1, 0)]
         for pair in range(1, 4):
-            plan.append(("wp", 2 * pair, 0))
-            plan.append(("wp", 2 * pair + 1, 0))
+            plan.append(("wp", pair, 0))
+            if pair == 1:
+                plan.append(("c", 0, 0))
+            plan.append(("wp", pair, 1))
             plan.append(("c", pair, 0))
         for col_half in range(2):
             for pair in range(4):
@@ -58,31 +60,32 @@ def tile_mixedrepeatheads_kernel(
         loaded = {}
         x_rows = x.rearrange("(p s) k -> p s k", s=4)
 
-        def wproj_rows(head):
-            return W_proj[head].rearrange("(g p j) c -> p g (j c)", g=4, p=P, j=4)
+        def wproj_rows(pair, g):
+            return W_proj[2 * pair : 2 * pair + 2, 512 * g : 512 * g + 512, :].rearrange(
+                "h (p j) c -> p h (j c)", j=4
+            )
 
         def issue(kind, a, b):
             if kind == "x":
                 raw = raw_pool.tile([P, 4096], BF16, tag="raw")
-                nc.sync.dma_start(
-                    out=raw[:].rearrange("p (s k) -> p s k", s=2), in_=x_rows[:, 2 * a : 2 * a + 2, :]
-                )
+                for within in range(2):
+                    nc.sync.dma_start(
+                        out=raw[:, within * 2048 : within * 2048 + 2048],
+                        in_=x_rows[:, 2 * a + within, :],
+                    )
                 loaded[(kind, a, b)] = raw
             elif kind == "wp":
                 raw = raw_pool.tile([P, 4096], BF16, tag="raw")
-                loaded[(kind, a, b)] = raw
-                if a >= 2:
-                    nc.sync.dma_start(
-                        out=raw[:].rearrange("p (g y) -> p g y", g=4), in_=wproj_rows(a)
-                    )
-                elif a == 1:
-                    for g in range(4):
+                by_head = raw[:].rearrange("p (g h y) -> p g h y", g=2, h=2)
+                for within in range(2):
+                    rows = wproj_rows(a, 2 * b + within)
+                    if a == 0:
                         for head in range(2):
-                            nc.sync.dma_start(
-                                out=loaded[("wp", head, 0)][:, g * 1024 : g * 1024 + 1024],
-                                in_=wproj_rows(head)[:, g, :],
-                            )
-                        load_small_rows(g)
+                            nc.sync.dma_start(out=by_head[:, within, head, :], in_=rows[:, head, :])
+                        load_small_rows(2 * b + within)
+                    else:
+                        nc.sync.dma_start(out=by_head[:, within, :, :], in_=rows)
+                loaded[(kind, a, b)] = raw
             elif kind == "wo":
                 raw = raw_pool.tile([P, 4096], BF16, tag="raw")
                 nc.sync.dma_start(
@@ -152,18 +155,17 @@ def tile_mixedrepeatheads_kernel(
 
         issue_until(RAW_BUFS)
 
-        w_col = const.tile([P, 4], F32)
-        b_col = const.tile([P, 4], F32)
+        scalars = const.tile([P, 3, 4], F32)
+        w_col = scalars[:, 0, :]
         clipped = const.tile([P, 4], F32)
         root = const.tile([P, 4], F32)
         decay = const.tile([P, 4], F32)
         coef = const.tile([P, 4], F32)
+        b_proj_cols = const.tile([P, 4, 4], F32)
         bias = const.tile([P, 4, 4], F32)
 
-        def prepare_small_vectors():
+        def spread_small_vectors():
             spread = psum.tile([P, 512], F32, tag="bank")
-            at_b = COL_B - COL_W
-            at_decay = COL_DECAY - COL_W
             nc.tensor.matmul(
                 out=spread[:, 0:64],
                 lhsT=ones[:],
@@ -180,39 +182,49 @@ def tile_mixedrepeatheads_kernel(
                 )
             for head in range(2):
                 part = slice(64 * head, 64 * head + 64)
-                nc.vector.tensor_copy(out=w_col[part, :], in_=spread[part, head:8:2])
                 nc.vector.tensor_copy(
-                    out=b_col[part, :], in_=spread[part, at_b + head : at_b + 8 : 2]
+                    out=scalars[part, :, :],
+                    in_=spread[part, 0:48].rearrange("m (a y) -> m a y", y=16)[:, :, head:8:2],
                 )
-                nc.vector.tensor_scalar(
-                    out=clipped[part, :],
-                    in0=spread[part, at_decay + head : at_decay + 8 : 2],
-                    scalar1=0.9,
-                    scalar2=1.0,
-                    op0=ALU.max,
-                    op1=ALU.min,
-                )
-            nc.scalar.sqrt(root[:], clipped[:])
-            nc.scalar.sqrt(decay[:], root[:])
-            b_proj_t = spread[:, 128:384].bitcast(BF16).rearrange("m (v r e) -> m v r e", v=2, e=2)
+            nc.vector.tensor_copy(
+                out=b_proj_cols[:].rearrange("m r (v e) -> m r v e", v=2),
+                in_=spread[:, 128:384]
+                .bitcast(BF16)
+                .rearrange("m (v r e) -> m r v e", v=2, e=2)[:, 0:4, :, :],
+            )
+        def spread_b_out():
+            for half in range(2):
+                repeated = psum.tile([P, 1024], BF16, tag="bank")
+                for quarter in range(2):
+                    first = half * 1024 + quarter * 512
+                    nc.tensor.matmul(
+                        out=repeated[:, quarter * 512 : quarter * 512 + 512],
+                        lhsT=ones[:],
+                        rhs=small[:, first : first + 512],
+                        start=True,
+                        stop=True,
+                    )
+                copy_on(SCALAR, b_out_all[:, half * 1024 : half * 1024 + 1024], repeated[:])
+
+        def combine_small_vectors():
+            nc.gpsimd.tensor_scalar(
+                out=clipped[:], in0=scalars[:, 2, :], scalar1=0.9, scalar2=1.0, op0=ALU.max, op1=ALU.min
+            )
             for pair in range(4):
-                nc.vector.tensor_scalar(
-                    out=bias[:, pair, :].rearrange("m (v e) -> m v e", v=2),
-                    in0=b_proj_t[:, :, pair, :],
-                    scalar1=w_col[:, pair : pair + 1],
-                    scalar2=b_col[:, pair : pair + 1],
+                nc.gpsimd.tensor_scalar(
+                    out=bias[:, pair, :],
+                    in0=b_proj_cols[:, pair, :],
+                    scalar1=scalars[:, 0, pair : pair + 1],
+                    scalar2=scalars[:, 1, pair : pair + 1],
                     op0=ALU.mult,
                     op1=ALU.add,
                 )
-            nc.vector.tensor_mul(coef[:, 0:2], w_col[:, 0:2], decay[:, 0:2])
-            nc.vector.tensor_copy(out=coef[:, 2:4], in_=decay[:, 2:4])
-            for panel in range(4):
-                cols = slice(panel * 512, panel * 512 + 512)
-                repeated = psum.tile([P, 512], F32, tag="bank")
-                nc.tensor.matmul(
-                    out=repeated[:], lhsT=ones[:], rhs=small[:, cols], start=True, stop=True
-                )
-                copy_on(panel % 2, b_out_all[:, cols], repeated[:])
+            nc.scalar.sqrt(root[:], clipped[:])
+            nc.scalar.sqrt(decay[:], root[:])
+            nc.gpsimd.tensor_tensor(
+                out=coef[:, 0:2], in0=w_col[:, 0:2], in1=decay[:, 0:2], op=ALU.mult
+            )
+            nc.gpsimd.tensor_copy(out=coef[:, 2:4], in_=decay[:, 2:4])
 
         x_words = const.tile([P, 4, 512], U32, align_bytes=64)
         x_scales = const.tile([P, 4, 512], U8, align_bytes=64)
@@ -240,40 +252,51 @@ def tile_mixedrepeatheads_kernel(
             else:
                 nc.scalar.copy(out=dst, in_=src)
 
-        def transpose_x(x_half, g):
-            x_f32 = loaded[("x", x_half, 0)][:].bitcast(F32)
-            bank = new_bank(("x", x_half, g))
-            for u in range(2):
-                for within in range(2):
-                    first = within * 1024 + 256 * g
-                    nc.tensor.transpose(
-                        bank[:, u * 256 + within * 128 : u * 256 + within * 128 + 128],
-                        x_f32[:, first + u : first + 256 : 2],
-                        ident[:],
-                    )
-            copy_on(
-                (g + 1) % 2,
-                grouped_tile(("x", g))[:].bitcast(F32).rearrange("q (r u) -> q r u", u=2)[
-                    :, x_half * 256 : x_half * 256 + 256, :
-                ],
-                bank[:].rearrange("q (u r) -> q r u", u=2),
-            )
+        x_grouped = []
+        for half in range(2):
+            x_tile = addend_pool.tile([P, 2, 2048], BF16, tag="addend", align_bytes=64)
+            x_grouped.append(x_tile)
 
-        def quantise_x(g):
-            nc.vector.quantize_mx(
-                out=x_words[:, g, :].bitcast(FP8X4),
-                scales=x_scales[:, g, :],
-                in_=grouped_tile(("x", g))[:],
-            )
+        def transpose_x(s):
+            x_half, within = divmod(s, 2)
+            x_f32 = loaded[("x", x_half, 0)][:].bitcast(F32)
+            for g in range(4):
+                if g % 2 == 0:
+                    bank = new_bank(("x", s, g // 2))
+                for u in range(2):
+                    first = within * 1024 + 256 * g
+                    at = (g % 2) * 256 + u * 128
+                    nc.tensor.transpose(
+                        bank[:, at : at + 128], x_f32[:, first + u : first + 256 : 2], ident[:]
+                    )
+
+        def copy_x(s):
+            for half in range(2):
+                copy_on(
+                    SCALAR if half == 0 else VECTOR,
+                    x_grouped[half][:].bitcast(F32).rearrange("q g (r u) -> q g r u", u=2)[
+                        :, :, s * 128 : s * 128 + 128, :
+                    ],
+                    live[("x", s, half)][:].rearrange("q (g u r) -> q g r u", g=2, u=2),
+                )
+
+        def quantise_x(first, count):
+            for g in range(4):
+                nc.vector.quantize_mx(
+                    out=x_words[:, g, first * 128 : (first + count) * 128].bitcast(FP8X4),
+                    scales=x_scales[:, g, first * 128 : (first + count) * 128],
+                    in_=x_grouped[g // 2][:, g % 2, first * 512 : (first + count) * 512],
+                )
 
         def regroup_wproj(pair, g):
             dst = grouped_tile(("wproj", pair, g))[:].rearrange("p (t m j) -> p t m j", t=4, m=P, j=4)
             for head in range(2):
-                src = loaded[("wp", 2 * pair + head, 0)][:, g * 1024 : g * 1024 + 1024].rearrange(
+                first = (g % 2) * 2048 + head * 1024
+                src = loaded[("wp", pair, g // 2)][:, first : first + 1024].rearrange(
                     "p (j m t) -> p m j t", j=4, m=64, t=4
                 )
                 copy_on(
-                    (g + head) % 2,
+                    SCALAR if head == 0 else VECTOR,
                     dst[:, :, 64 * head : 64 * head + 64, :].rearrange("p t m j -> p m j t"),
                     src,
                 )
@@ -299,7 +322,7 @@ def tile_mixedrepeatheads_kernel(
                 )
 
         def scale_caches(pair):
-            addend = addend_pool.tile([P, 4, 512], F32, tag="addend")
+            addend = addend_pool.tile([P, 4, 512], F32, tag="addend", align_bytes=64)
             live[("addend", pair)] = addend
             for v in range(2):
                 halves = live[("caches", pair, v)][:].bitcast(BF16).rearrange("m (r e) -> m r e", e=2)
@@ -407,16 +430,16 @@ def tile_mixedrepeatheads_kernel(
             quantise_wproj(0, g - 1)
         quantise_wproj(0, 3)
         raw_tiles_read(2)
-        prepare_small_vectors()
-        for x_half in range(2):
-            for g in range(4):
-                transpose_x(x_half, g)
-            raw_tiles_read(1)
-        for g in range(4):
-            quantise_x(g)
-        transpose_caches(0, 0)
-        transpose_caches(0, 1)
-        scale_caches(0)
+        spread_b_out()
+        spread_small_vectors()
+        for s in range(4):
+            transpose_x(s)
+            copy_x(s)
+            if s % 2 == 1:
+                quantise_x(s - 1, 2)
+                raw_tiles_read(1)
+            if s == 1:
+                combine_small_vectors()
 
         for pair in range(1, 4):
             before = pair - 1
@@ -424,14 +447,19 @@ def tile_mixedrepeatheads_kernel(
             if pair >= 2:
                 quantise_hidden(pair - 2)
             regroup_wproj(pair, 1)
+            raw_tiles_read(1)
             quantise_wproj(pair, 0)
             project(before, 0)
+            if pair == 1:
+                transpose_caches(0, 0)
+                transpose_caches(0, 1)
+                scale_caches(0)
             regroup_wproj(pair, 2)
             quantise_wproj(pair, 1)
             mix(before, 0)
             project(before, 1)
             regroup_wproj(pair, 3)
-            raw_tiles_read(2)
+            raw_tiles_read(1)
             quantise_wproj(pair, 2)
             mix(before, 1)
             transpose_caches(pair, 0)

@@ -19,7 +19,9 @@ SCALAR = 1
 
 RAW_BUFS = 8
 
-WOUT_VECTOR_COLS = (128, 128, 112, 96)
+PANELS = ((0, 512, 128), (512, 512, 128), (1024, 512, 112), (1536, 512, 96))
+
+BESIDE = ((0, 1), (2,), (3,), ())
 
 COL_W = 2048
 COL_B = 2064
@@ -159,7 +161,6 @@ def tile_mixedrepeatheads_kernel(
         w_col = scalars[:, 0, :]
         clipped = const.tile([P, 4], F32)
         root = const.tile([P, 4], F32)
-        decay = const.tile([P, 4], F32)
         coef = const.tile([P, 4], F32)
         b_proj_cols = const.tile([P, 4, 4], F32)
         bias = const.tile([P, 4, 4], F32)
@@ -192,6 +193,10 @@ def tile_mixedrepeatheads_kernel(
                 .bitcast(BF16)
                 .rearrange("m (v r e) -> m r v e", v=2, e=2)[:, 0:4, :, :],
             )
+            nc.vector.tensor_scalar(
+                out=clipped[:], in0=scalars[:, 2, :], scalar1=0.9, scalar2=1.0, op0=ALU.max, op1=ALU.min
+            )
+
         def spread_b_out():
             for half in range(2):
                 repeated = psum.tile([P, 1024], BF16, tag="bank")
@@ -207,31 +212,30 @@ def tile_mixedrepeatheads_kernel(
                 copy_on(SCALAR, b_out_all[:, half * 1024 : half * 1024 + 1024], repeated[:])
 
         def combine_small_vectors():
-            nc.gpsimd.tensor_scalar(
-                out=clipped[:], in0=scalars[:, 2, :], scalar1=0.9, scalar2=1.0, op0=ALU.max, op1=ALU.min
-            )
-            for pair in range(4):
-                nc.gpsimd.tensor_scalar(
-                    out=bias[:, pair, :],
-                    in0=b_proj_cols[:, pair, :],
-                    scalar1=scalars[:, 0, pair : pair + 1],
-                    scalar2=scalars[:, 1, pair : pair + 1],
-                    op0=ALU.mult,
-                    op1=ALU.add,
-                )
             nc.scalar.sqrt(root[:], clipped[:])
-            nc.scalar.sqrt(decay[:], root[:])
-            nc.gpsimd.tensor_tensor(
-                out=coef[:, 0:2], in0=w_col[:, 0:2], in1=decay[:, 0:2], op=ALU.mult
+            nc.scalar.sqrt(coef[:], root[:])
+            nc.vector.tensor_tensor(
+                out=bias[:],
+                in0=b_proj_cols[:],
+                in1=scalars[:, 0, :].unsqueeze(2).to_broadcast([P, 4, 4]),
+                op=ALU.mult,
             )
-            nc.gpsimd.tensor_copy(out=coef[:, 2:4], in_=decay[:, 2:4])
+
+        def finish_small_vectors():
+            nc.vector.tensor_tensor(
+                out=bias[:],
+                in0=bias[:],
+                in1=scalars[:, 1, :].unsqueeze(2).to_broadcast([P, 4, 4]),
+                op=ALU.add,
+            )
+            nc.vector.tensor_mul(coef[:, 0:2], coef[:, 0:2], w_col[:, 0:2])
 
         x_words = const.tile([P, 4, 512], U32, align_bytes=64)
         x_scales = const.tile([P, 4, 512], U8, align_bytes=64)
         hidden_words = const.tile([P, 4, 512], U32, align_bytes=64)
         hidden_scales = const.tile([P, 4, 512], U8, align_bytes=64)
-        wout_words = const.tile([P, 16, 512], U32, align_bytes=64)
-        wout_scales = const.tile([P, 16, 512], U8, align_bytes=64)
+        wout_words = const.tile([P, 4, 2048], U32, align_bytes=64)
+        wout_scales = const.tile([P, 4, 2048], U8, align_bytes=64)
 
         live = {}
 
@@ -372,34 +376,37 @@ def tile_mixedrepeatheads_kernel(
             )
 
         def regroup_wout(panel, pair):
-            rows = loaded[("wo", panel // 2, pair)][:].rearrange("p (j n) -> p j n", j=4)
-            first = (panel % 2) * 512
-            dst = grouped_tile(("wout", panel, pair))[:].rearrange("p (n j) -> p n j", j=4)
-            cut = WOUT_VECTOR_COLS[panel]
-            for lo, hi, engine in ((0, cut, VECTOR), (cut, 512, SCALAR)):
-                copy_on(
-                    engine,
-                    dst[:, lo:hi, :].rearrange("p (f i) j -> p f j i", i=4),
-                    rows[:, :, first + lo : first + hi].rearrange("p j (f i) -> p f j i", i=4),
-                )
+            first, width, cut = PANELS[panel]
+            rows = loaded[("wo", first // 1024, pair)][:].rearrange("p (j n) -> p j n", j=4)
+            at = first % 1024
+            dst = grouped_tile(("wout", panel, pair))[:, 0 : 4 * width].rearrange("p (n j) -> p n j", j=4)
+            for lo, hi, engine in ((0, cut, VECTOR), (cut, width, SCALAR)):
+                if hi > lo:
+                    copy_on(
+                        engine,
+                        dst[:, lo:hi, :].rearrange("p (f i) j -> p f j i", i=4),
+                        rows[:, :, at + lo : at + hi].rearrange("p j (f i) -> p f j i", i=4),
+                    )
 
         def quantise_wout(panel, pair):
+            first, width, cut = PANELS[panel]
             nc.vector.quantize_mx(
-                out=wout_words[:, panel * 4 + pair, :].bitcast(FP8X4),
-                scales=wout_scales[:, panel * 4 + pair, :],
-                in_=grouped_tile(("wout", panel, pair))[:],
+                out=wout_words[:, pair, first : first + width].bitcast(FP8X4),
+                scales=wout_scales[:, pair, first : first + width],
+                in_=grouped_tile(("wout", panel, pair))[:, 0 : 4 * width],
             )
 
         def multiply_out(panel, pair):
+            first, width, cut = PANELS[panel]
             for s in range(4):
                 if pair == 0:
                     new_bank(("out", panel, s))
                 nc.tensor.matmul_mx(
-                    out=live[("out", panel, s)][:],
+                    out=live[("out", panel, s)][:, 0:width],
                     lhsT=hidden_words[:, pair, s * 128 : s * 128 + 128].bitcast(FP8X4),
                     lhsT_scale=hidden_scales[:, pair, s * 128 : s * 128 + 128],
-                    rhs=wout_words[:, panel * 4 + pair, :].bitcast(FP8X4),
-                    rhs_scale=wout_scales[:, panel * 4 + pair, :],
+                    rhs=wout_words[:, pair, first : first + width].bitcast(FP8X4),
+                    rhs_scale=wout_scales[:, pair, first : first + width],
                     start=(pair == 0),
                     stop=(pair == 3),
                 )
@@ -407,20 +414,22 @@ def tile_mixedrepeatheads_kernel(
         out_rows = out.rearrange("(p s) n -> p s n", s=4)
 
         def add_b_out(panel, s):
+            first, width, cut = PANELS[panel]
             if ("result", panel) not in live:
                 result = result_pool.tile([P, 4, 512], F32, tag="result")
                 live[("result", panel)] = result
             nc.vector.tensor_tensor(
-                out=live[("result", panel)][:, s, :],
-                in0=live[("out", panel, s)][:],
-                in1=b_out_all[:, panel * 512 : panel * 512 + 512],
+                out=live[("result", panel)][:, s, 0:width],
+                in0=live[("out", panel, s)][:, 0:width],
+                in1=b_out_all[:, first : first + width],
                 op=ALU.add,
             )
 
         def store(panel, s0, s1):
+            first, width, cut = PANELS[panel]
             nc.sync.dma_start(
-                out=out_rows[:, s0:s1, panel * 512 : panel * 512 + 512],
-                in_=live[("result", panel)][:, s0:s1, :],
+                out=out_rows[:, s0:s1, first : first + width],
+                in_=live[("result", panel)][:, s0:s1, 0:width],
             )
 
 
@@ -440,6 +449,7 @@ def tile_mixedrepeatheads_kernel(
                 raw_tiles_read(1)
             if s == 1:
                 combine_small_vectors()
+        finish_small_vectors()
 
         for pair in range(1, 4):
             before = pair - 1
@@ -471,18 +481,16 @@ def tile_mixedrepeatheads_kernel(
             mix(before, 3)
             scale_caches(pair)
 
-        def beside(panel, s):
-            if panel == 0:
-                project(3, s)
-                mix(3, s)
-                if s == 3:
-                    quantise_hidden(3)
-            else:
-                add_b_out(panel - 1, s)
-                if s % 2 == 1:
-                    store(panel - 1, s - 1, s + 1)
+        LAST = len(PANELS) - 1
 
-        for panel in range(4):
+        def finish(panel, s):
+            add_b_out(panel, s)
+            if panel == LAST:
+                store(panel, s, s + 1)
+            elif s % 2 == 1:
+                store(panel, s - 1, s + 1)
+
+        for panel in range(LAST + 1):
             regroup_wout(panel, 0)
             if panel == 0:
                 quantise_hidden(2)
@@ -490,16 +498,16 @@ def tile_mixedrepeatheads_kernel(
                 if pair < 3:
                     regroup_wout(panel, pair + 1)
                 quantise_wout(panel, pair)
-                if pair < 3:
-                    if panel > 0:
-                        multiply_out(panel, pair)
-                    beside(panel, pair)
-            beside(panel, 3)
+                if panel == 0:
+                    project(3, pair)
+                    mix(3, pair)
+                else:
+                    multiply_out(panel, pair)
+                    for s in BESIDE[pair]:
+                        finish(panel - 1, s)
             if panel == 0:
+                quantise_hidden(3)
                 for pair in range(4):
                     multiply_out(0, pair)
-            else:
-                multiply_out(panel, 3)
         for s in range(4):
-            add_b_out(3, s)
-            store(3, s, s + 1)
+            finish(LAST, s)

@@ -19,7 +19,7 @@ SCALAR = 1
 
 RAW_BUFS = 8
 
-PANELS = ((0, 512, 128), (512, 512, 128), (1024, 512, 112), (1536, 512, 96))
+PANELS = ((0, 512, (0, 240, 0, 240)), (512, 512, (0, 240, 0, 240)), (1024, 512, (0, 224, 0, 224)), (1536, 512, (0, 192, 0, 224)))
 
 BESIDE = ((0, 1), (2,), (3,), ())
 
@@ -230,8 +230,8 @@ def tile_mixedrepeatheads_kernel(
             )
             nc.vector.tensor_mul(coef[:, 0:2], coef[:, 0:2], w_col[:, 0:2])
 
-        x_words = const.tile([P, 4, 512], U32, align_bytes=64)
-        x_scales = const.tile([P, 4, 512], U8, align_bytes=64)
+        x_words = const.tile([P, 2, 4, 256], U32, align_bytes=64)
+        x_scales = const.tile([P, 2, 4, 256], U8, align_bytes=64)
         hidden_words = const.tile([P, 4, 512], U32, align_bytes=64)
         hidden_scales = const.tile([P, 4, 512], U8, align_bytes=64)
         wout_words = const.tile([P, 4, 2048], U32, align_bytes=64)
@@ -257,8 +257,8 @@ def tile_mixedrepeatheads_kernel(
                 nc.scalar.copy(out=dst, in_=src)
 
         x_grouped = []
-        for half in range(2):
-            x_tile = addend_pool.tile([P, 2, 2048], BF16, tag="addend", align_bytes=64)
+        for x_half in range(2):
+            x_tile = addend_pool.tile([P, 4, 1024], BF16, tag="addend", align_bytes=64)
             x_grouped.append(x_tile)
 
         def transpose_x(s):
@@ -275,21 +275,23 @@ def tile_mixedrepeatheads_kernel(
                     )
 
         def copy_x(s):
+            x_half, within = divmod(s, 2)
             for half in range(2):
                 copy_on(
                     SCALAR if half == 0 else VECTOR,
-                    x_grouped[half][:].bitcast(F32).rearrange("q g (r u) -> q g r u", u=2)[
-                        :, :, s * 128 : s * 128 + 128, :
+                    x_grouped[x_half][:].bitcast(F32).rearrange("q g (r u) -> q g r u", u=2)[
+                        :, 2 * half : 2 * half + 2, within * 128 : within * 128 + 128, :
                     ],
                     live[("x", s, half)][:].rearrange("q (g u r) -> q g r u", g=2, u=2),
                 )
 
-        def quantise_x(first, count):
-            for g in range(4):
+        def quantise_x(x_half):
+            for half in range(2):
+                passes = slice(2 * half, 2 * half + 2)
                 nc.vector.quantize_mx(
-                    out=x_words[:, g, first * 128 : (first + count) * 128].bitcast(FP8X4),
-                    scales=x_scales[:, g, first * 128 : (first + count) * 128],
-                    in_=x_grouped[g // 2][:, g % 2, first * 512 : (first + count) * 512],
+                    out=x_words[:, x_half, passes, :].rearrange("p g r -> p (g r)").bitcast(FP8X4),
+                    scales=x_scales[:, x_half, passes, :].rearrange("p g r -> p (g r)"),
+                    in_=x_grouped[x_half][:, passes, :].rearrange("p g y -> p (g y)"),
                 )
 
         def regroup_wproj(pair, g):
@@ -344,14 +346,15 @@ def tile_mixedrepeatheads_kernel(
             bank = new_bank(("proj", pair, s))
             w_words = live[("wproj words", pair)]
             w_scales = live[("wproj scales", pair)]
+            rows = slice((s % 2) * 128, (s % 2) * 128 + 128)
             for t in range(4):
                 for g in range(4):
                     nc.tensor.matmul_mx(
                         out=bank[:, t * 128 : t * 128 + 128],
                         lhsT=w_words[:, g, t * 128 : t * 128 + 128].bitcast(FP8X4),
                         lhsT_scale=w_scales[:, g, t * 128 : t * 128 + 128],
-                        rhs=x_words[:, g, s * 128 : s * 128 + 128].bitcast(FP8X4),
-                        rhs_scale=x_scales[:, g, s * 128 : s * 128 + 128],
+                        rhs=x_words[:, s // 2, g, rows].bitcast(FP8X4),
+                        rhs_scale=x_scales[:, s // 2, g, rows],
                         start=(g == 0),
                         stop=(g == 3),
                     )
@@ -376,7 +379,8 @@ def tile_mixedrepeatheads_kernel(
             )
 
         def regroup_wout(panel, pair):
-            first, width, cut = PANELS[panel]
+            first, width, cuts = PANELS[panel]
+            cut = cuts[pair]
             rows = loaded[("wo", first // 1024, pair)][:].rearrange("p (j n) -> p j n", j=4)
             at = first % 1024
             dst = grouped_tile(("wout", panel, pair))[:, 0 : 4 * width].rearrange("p (n j) -> p n j", j=4)
@@ -445,7 +449,7 @@ def tile_mixedrepeatheads_kernel(
             transpose_x(s)
             copy_x(s)
             if s % 2 == 1:
-                quantise_x(s - 1, 2)
+                quantise_x(s // 2)
                 raw_tiles_read(1)
             if s == 1:
                 combine_small_vectors()

from contextlib import ExitStack

import concourse.masks as masks
import concourse.mybir as mybir

F32 = mybir.dt.float32
BF16 = mybir.dt.bfloat16
U32 = mybir.dt.uint32
U8 = mybir.dt.uint8
FP8X4 = mybir.dt.float8_e4m3fn_x4
ALU = mybir.AluOpType
ACT = mybir.ActivationFunctionType

P = 128
FLOPS = 2 * 512 * 2048 * 2048 * 2

VECTOR = 0
SCALAR = 1

RAW_BUFS = 8

PANELS = ((0, 512, (0, 240, 0, 240)), (512, 512, (0, 240, 0, 240)), (1024, 512, (0, 224, 0, 224)), (1536, 512, (0, 192, 0, 224)))

BESIDE = ((0, 1), (2,), (3,), ())

COL_W = 2048
COL_B = 2064
COL_DECAY = 2080
COL_HEADS_END = 2112
COL_B_PROJ = 2112
SMALL_COLS = 2624


def tile_mixedrepeatheads_kernel(
    tc, x, index, W_proj, b_proj, W_out, b_out, w_mix, b_mix, decay_values, caches, out
):
    nc = tc.nc
    with ExitStack() as ctx:
        ctx.enter_context(tc.manual_schedule())
        const = ctx.enter_context(tc.tile_pool(name="const", bufs=1))
        raw_pool = ctx.enter_context(tc.tile_pool(name="raw", bufs=RAW_BUFS))
        grouped_pool = ctx.enter_context(tc.tile_pool(name="grouped", bufs=6))
        caches_pool = ctx.enter_context(tc.tile_pool(name="caches", bufs=4))
        wproj_pool = ctx.enter_context(tc.tile_pool(name="wproj", bufs=2))
        addend_pool = ctx.enter_context(tc.tile_pool(name="addend", bufs=2))
        result_pool = ctx.enter_context(tc.tile_pool(name="result", bufs=2))
        psum = ctx.enter_context(tc.psum_pool(name="psum", bufs=8))

        b_out_all = const.tile([P, 2048], BF16)

        plan = [("wp", 0, 0), ("wp", 0, 1), ("x", 0, 0), ("x", 1, 0)]
        for pair in range(1, 4):
            plan.append(("wp", pair, 0))
            if pair == 1:
                plan.append(("c", 0, 0))
            plan.append(("wp", pair, 1))
            plan.append(("c", pair, 0))
        for col_half in range(2):
            for pair in range(4):
                plan.append(("wo", col_half, pair))
        progress = {"issued": 0, "raw_issued": 0, "raw_read": 0}
        loaded = {}
        x_rows = x.rearrange("(p s) k -> p s k", s=4)

        def wproj_rows(pair, g):
            return W_proj[2 * pair : 2 * pair + 2, 512 * g : 512 * g + 512, :].rearrange(
                "h (p j) c -> p h (j c)", j=4
            )

        def issue(kind, a, b):
            if kind == "x":
                raw = raw_pool.tile([P, 4096], BF16, tag="raw")
                for within in range(2):
                    nc.sync.dma_start(
                        out=raw[:, within * 2048 : within * 2048 + 2048],
                        in_=x_rows[:, 2 * a + within, :],
                    )
                loaded[(kind, a, b)] = raw
            elif kind == "wp":
                raw = raw_pool.tile([P, 4096], BF16, tag="raw")
                by_head = raw[:].rearrange("p (g h y) -> p g h y", g=2, h=2)
                for within in range(2):
                    rows = wproj_rows(a, 2 * b + within)
                    if a == 0:
                        for head in range(2):
                            nc.sync.dma_start(out=by_head[:, within, head, :], in_=rows[:, head, :])
                        load_small_rows(2 * b + within)
                    else:
                        nc.sync.dma_start(out=by_head[:, within, :, :], in_=rows)
                loaded[(kind, a, b)] = raw
            elif kind == "wo":
                raw = raw_pool.tile([P, 4096], BF16, tag="raw")
                nc.sync.dma_start(
                    out=raw[:].rearrange("p (j n) -> p j n", j=4),
                    in_=W_out[512 * b : 512 * b + 512, 1024 * a : 1024 * a + 1024].rearrange(
                        "(p j) n -> p j n", j=4
                    ),
                )
                loaded[(kind, a, b)] = raw
            else:
                raw = caches_pool.tile([P, 2048], BF16, tag="caches")
                by_group = raw[:].rearrange("p (s c) -> p s c", s=4)
                for head in range(2):
                    nc.sync.dma_start(
                        out=by_group[:, :, 256 * head : 256 * head + 256],
                        in_=caches[2 * a + head].rearrange("(p s) c -> p s c", s=4),
                    )
                loaded[(kind, a, b)] = raw

        def issue_until(raw_tiles):
            while progress["issued"] < len(plan):
                kind, a, b = plan[progress["issued"]]
                takes_raw_tile = kind in ("x", "wp", "wo")
                if takes_raw_tile and progress["raw_issued"] >= raw_tiles:
                    break
                issue(kind, a, b)
                progress["issued"] += 1
                if takes_raw_tile:
                    progress["raw_issued"] += 1

        def raw_tiles_read(count):
            progress["raw_read"] += count
            issue_until(progress["raw_read"] + RAW_BUFS)

        scratch = const.tile([P, 1], F32)
        nc.vector.memset(scratch[:], 1.0)
        nc.scalar.sqrt(scratch[:], scratch[:])

        small = const.tile([P, SMALL_COLS], BF16)
        ones = const.tile([P, P], BF16)
        nc.vector.memset(small[:].bitcast(F32), 0.0)
        nc.vector.memset(ones[:], 1.0)

        ident = const.tile([P, P], F32)
        masks.make_identity(nc, ident[:])

        def load_small_rows(step):
            with nc.allow_non_contiguous_dma(reason="eight scalars, one of each head"):
                if step == 0:
                    nc.sync.dma_start(out=small[0:1, 0:2048], in_=b_out.unsqueeze(0))
                elif step == 1:
                    nc.sync.dma_start(
                        out=small[0:1, COL_W : COL_W + 8], in_=w_mix[:, index].unsqueeze(0)
                    )
                elif step == 2:
                    nc.sync.dma_start(
                        out=small[0:1, COL_B : COL_B + 8], in_=b_mix[:, index].unsqueeze(0)
                    )
                else:
                    nc.sync.dma_start(
                        out=small[0:1, COL_DECAY : COL_DECAY + 8], in_=decay_values.unsqueeze(0)
                    )
                    nc.sync.dma_start(
                        out=small[0:4, COL_B_PROJ:SMALL_COLS],
                        in_=b_proj.rearrange("(a h) c -> a (h c)", h=2),
                    )

        issue_until(RAW_BUFS)

        scalars = const.tile([P, 3, 4], F32)
        w_col = scalars[:, 0, :]
        clipped = const.tile([P, 4], F32)
        root = const.tile([P, 4], F32)
        coef = const.tile([P, 4], F32)
        b_proj_cols = const.tile([P, 4, 4], F32)
        bias = const.tile([P, 4, 4], F32)

        def spread_small_vectors():
            spread = psum.tile([P, 512], F32, tag="bank")
            nc.tensor.matmul(
                out=spread[:, 0:64],
                lhsT=ones[:],
                rhs=small[:, COL_W:COL_HEADS_END],
                start=True,
                stop=True,
            )
            small_f32 = small[:].bitcast(F32)
            for v in range(2):
                nc.tensor.transpose(
                    spread[:, 128 + v * 128 : 256 + v * 128],
                    small_f32[:, COL_B_PROJ // 2 + v : SMALL_COLS // 2 : 2],
                    ident[:],
                )
            for head in range(2):
                part = slice(64 * head, 64 * head + 64)
                nc.vector.tensor_copy(
                    out=scalars[part, :, :],
                    in_=spread[part, 0:48].rearrange("m (a y) -> m a y", y=16)[:, :, head:8:2],
                )
            nc.vector.tensor_copy(
                out=b_proj_cols[:].rearrange("m r (v e) -> m r v e", v=2),
                in_=spread[:, 128:384]
                .bitcast(BF16)
                .rearrange("m (v r e) -> m r v e", v=2, e=2)[:, 0:4, :, :],
            )
            nc.vector.tensor_scalar(
                out=clipped[:], in0=scalars[:, 2, :], scalar1=0.9, scalar2=1.0, op0=ALU.max, op1=ALU.min
            )

        def spread_b_out():
            for half in range(2):
                repeated = psum.tile([P, 1024], BF16, tag="bank")
                for quarter in range(2):
                    first = half * 1024 + quarter * 512
                    nc.tensor.matmul(
                        out=repeated[:, quarter * 512 : quarter * 512 + 512],
                        lhsT=ones[:],
                        rhs=small[:, first : first + 512],
                        start=True,
                        stop=True,
                    )
                copy_on(SCALAR, b_out_all[:, half * 1024 : half * 1024 + 1024], repeated[:])

        def combine_small_vectors():
            nc.scalar.sqrt(root[:], clipped[:])
            nc.scalar.sqrt(coef[:], root[:])
            nc.vector.tensor_tensor(
                out=bias[:],
                in0=b_proj_cols[:],
                in1=scalars[:, 0, :].unsqueeze(2).to_broadcast([P, 4, 4]),
                op=ALU.mult,
            )

        def finish_small_vectors():
            nc.vector.tensor_tensor(
                out=bias[:],
                in0=bias[:],
                in1=scalars[:, 1, :].unsqueeze(2).to_broadcast([P, 4, 4]),
                op=ALU.add,
            )
            nc.vector.tensor_mul(coef[:, 0:2], coef[:, 0:2], w_col[:, 0:2])

        x_words = const.tile([P, 2, 4, 256], U32, align_bytes=64)
        x_scales = const.tile([P, 2, 4, 256], U8, align_bytes=64)
        hidden_words = const.tile([P, 4, 512], U32, align_bytes=64)
        hidden_scales = const.tile([P, 4, 512], U8, align_bytes=64)
        wout_words = const.tile([P, 4, 2048], U32, align_bytes=64)
        wout_scales = const.tile([P, 4, 2048], U8, align_bytes=64)

        live = {}

        def grouped_tile(key):
            if key not in live:
                grouped = grouped_pool.tile([P, 2048], BF16, tag="grouped", align_bytes=64)
                live[key] = grouped
            return live[key]

        def new_bank(key):
            bank = psum.tile([P, 512], F32, tag="bank")
            live[key] = bank
            return bank

        def copy_on(engine, dst, src):
            if engine == VECTOR:
                nc.vector.tensor_copy(out=dst, in_=src)
            else:
                nc.scalar.copy(out=dst, in_=src)

        x_grouped = []
        for x_half in range(2):
            x_tile = addend_pool.tile([P, 4, 1024], BF16, tag="addend", align_bytes=64)
            x_grouped.append(x_tile)

        def transpose_x(s):
            x_half, within = divmod(s, 2)
            x_f32 = loaded[("x", x_half, 0)][:].bitcast(F32)
            for g in range(4):
                if g % 2 == 0:
                    bank = new_bank(("x", s, g // 2))
                for u in range(2):
                    first = within * 1024 + 256 * g
                    at = (g % 2) * 256 + u * 128
                    nc.tensor.transpose(
                        bank[:, at : at + 128], x_f32[:, first + u : first + 256 : 2], ident[:]
                    )

        def copy_x(s):
            x_half, within = divmod(s, 2)
            for half in range(2):
                copy_on(
                    SCALAR if half == 0 else VECTOR,
                    x_grouped[x_half][:].bitcast(F32).rearrange("q g (r u) -> q g r u", u=2)[
                        :, 2 * half : 2 * half + 2, within * 128 : within * 128 + 128, :
                    ],
                    live[("x", s, half)][:].rearrange("q (g u r) -> q g r u", g=2, u=2),
                )

        def quantise_x(x_half):
            for half in range(2):
                passes = slice(2 * half, 2 * half + 2)
                nc.vector.quantize_mx(
                    out=x_words[:, x_half, passes, :].rearrange("p g r -> p (g r)").bitcast(FP8X4),
                    scales=x_scales[:, x_half, passes, :].rearrange("p g r -> p (g r)"),
                    in_=x_grouped[x_half][:, passes, :].rearrange("p g y -> p (g y)"),
                )

        def regroup_wproj(pair, g):
            dst = grouped_tile(("wproj", pair, g))[:].rearrange("p (t m j) -> p t m j", t=4, m=P, j=4)
            for head in range(2):
                first = (g % 2) * 2048 + head * 1024
                src = loaded[("wp", pair, g // 2)][:, first : first + 1024].rearrange(
                    "p (j m t) -> p m j t", j=4, m=64, t=4
                )
                copy_on(
                    SCALAR if head == 0 else VECTOR,
                    dst[:, :, 64 * head : 64 * head + 64, :].rearrange("p t m j -> p m j t"),
                    src,
                )

        def quantise_wproj(pair, g):
            if ("wproj words", pair) not in live:
                wproj_words = wproj_pool.tile([P, 4, 512], U32, tag="words", align_bytes=64)
                wproj_scales = wproj_pool.tile([P, 4, 512], U8, tag="scales", align_bytes=64)
                live[("wproj words", pair)] = wproj_words
                live[("wproj scales", pair)] = wproj_scales
            nc.vector.quantize_mx(
                out=live[("wproj words", pair)][:, g, :].bitcast(FP8X4),
                scales=live[("wproj scales", pair)][:, g, :],
                in_=grouped_tile(("wproj", pair, g))[:],
            )

        def transpose_caches(pair, v):
            caches_f32 = loaded[("c", pair, 0)][:].bitcast(F32).rearrange("p (s w) -> p s w", s=4)
            bank = new_bank(("caches", pair, v))
            for s in range(4):
                nc.tensor.transpose(
                    bank[:, s * 128 : s * 128 + 128], caches_f32[:, s, v : 256 : 2], ident[:]
                )

        def scale_caches(pair):
            addend = addend_pool.tile([P, 4, 512], F32, tag="addend", align_bytes=64)
            live[("addend", pair)] = addend
            for v in range(2):
                halves = live[("caches", pair, v)][:].bitcast(BF16).rearrange("m (r e) -> m r e", e=2)
                for e in range(2):
                    t = 2 * v + e
                    nc.scalar.activation(
                        out=addend[:, t, :],
                        in_=halves[:, :, e],
                        func=ACT.Identity,
                        bias=bias[:, pair, t : t + 1],
                        scale=coef[:, pair : pair + 1],
                    )

        def project(pair, s):
            bank = new_bank(("proj", pair, s))
            w_words = live[("wproj words", pair)]
            w_scales = live[("wproj scales", pair)]
            rows = slice((s % 2) * 128, (s % 2) * 128 + 128)
            for t in range(4):
                for g in range(4):
                    nc.tensor.matmul_mx(
                        out=bank[:, t * 128 : t * 128 + 128],
                        lhsT=w_words[:, g, t * 128 : t * 128 + 128].bitcast(FP8X4),
                        lhsT_scale=w_scales[:, g, t * 128 : t * 128 + 128],
                        rhs=x_words[:, s // 2, g, rows].bitcast(FP8X4),
                        rhs_scale=x_scales[:, s // 2, g, rows],
                        start=(g == 0),
                        stop=(g == 3),
                    )

        def mix(pair, s):
            nc.vector.scalar_tensor_tensor(
                out=grouped_tile(("hidden", pair))[:, s * 512 : s * 512 + 512].rearrange(
                    "m (r t) -> m r t", t=4
                ),
                in0=live[("proj", pair, s)][:].rearrange("m (t r) -> m r t", t=4),
                scalar=w_col[:, pair : pair + 1],
                in1=live[("addend", pair)][:, :, s * 128 : s * 128 + 128].rearrange("m t r -> m r t"),
                op0=ALU.mult,
                op1=ALU.add,
            )

        def quantise_hidden(pair):
            nc.vector.quantize_mx(
                out=hidden_words[:, pair, :].bitcast(FP8X4),
                scales=hidden_scales[:, pair, :],
                in_=grouped_tile(("hidden", pair))[:],
            )

        def regroup_wout(panel, pair):
            first, width, cuts = PANELS[panel]
            cut = cuts[pair]
            rows = loaded[("wo", first // 1024, pair)][:].rearrange("p (j n) -> p j n", j=4)
            at = first % 1024
            dst = grouped_tile(("wout", panel, pair))[:, 0 : 4 * width].rearrange("p (n j) -> p n j", j=4)
            for lo, hi, engine in ((0, cut, VECTOR), (cut, width, SCALAR)):
                if hi > lo:
                    copy_on(
                        engine,
                        dst[:, lo:hi, :].rearrange("p (f i) j -> p f j i", i=4),
                        rows[:, :, at + lo : at + hi].rearrange("p j (f i) -> p f j i", i=4),
                    )

        def quantise_wout(panel, pair):
            first, width, cut = PANELS[panel]
            nc.vector.quantize_mx(
                out=wout_words[:, pair, first : first + width].bitcast(FP8X4),
                scales=wout_scales[:, pair, first : first + width],
                in_=grouped_tile(("wout", panel, pair))[:, 0 : 4 * width],
            )

        def multiply_out(panel, pair):
            first, width, cut = PANELS[panel]
            for s in range(4):
                if pair == 0:
                    new_bank(("out", panel, s))
                nc.tensor.matmul_mx(
                    out=live[("out", panel, s)][:, 0:width],
                    lhsT=hidden_words[:, pair, s * 128 : s * 128 + 128].bitcast(FP8X4),
                    lhsT_scale=hidden_scales[:, pair, s * 128 : s * 128 + 128],
                    rhs=wout_words[:, pair, first : first + width].bitcast(FP8X4),
                    rhs_scale=wout_scales[:, pair, first : first + width],
                    start=(pair == 0),
                    stop=(pair == 3),
                )

        out_rows = out.rearrange("(p s) n -> p s n", s=4)

        def add_b_out(panel, s):
            first, width, cut = PANELS[panel]
            if ("result", panel) not in live:
                result = result_pool.tile([P, 4, 512], F32, tag="result")
                live[("result", panel)] = result
            nc.vector.tensor_tensor(
                out=live[("result", panel)][:, s, 0:width],
                in0=live[("out", panel, s)][:, 0:width],
                in1=b_out_all[:, first : first + width],
                op=ALU.add,
            )

        def store(panel, s0, s1):
            first, width, cut = PANELS[panel]
            nc.sync.dma_start(
                out=out_rows[:, s0:s1, first : first + width],
                in_=live[("result", panel)][:, s0:s1, 0:width],
            )


        regroup_wproj(0, 0)
        for g in range(1, 4):
            regroup_wproj(0, g)
            quantise_wproj(0, g - 1)
        quantise_wproj(0, 3)
        raw_tiles_read(2)
        spread_b_out()
        spread_small_vectors()
        for s in range(4):
            transpose_x(s)
            copy_x(s)
            if s % 2 == 1:
                quantise_x(s // 2)
                raw_tiles_read(1)
            if s == 1:
                combine_small_vectors()
        finish_small_vectors()

        for pair in range(1, 4):
            before = pair - 1
            regroup_wproj(pair, 0)
            if pair >= 2:
                quantise_hidden(pair - 2)
            regroup_wproj(pair, 1)
            raw_tiles_read(1)
            quantise_wproj(pair, 0)
            project(before, 0)
            if pair == 1:
                transpose_caches(0, 0)
                transpose_caches(0, 1)
                scale_caches(0)
            regroup_wproj(pair, 2)
            quantise_wproj(pair, 1)
            mix(before, 0)
            project(before, 1)
            regroup_wproj(pair, 3)
            raw_tiles_read(1)
            quantise_wproj(pair, 2)
            mix(before, 1)
            transpose_caches(pair, 0)
            transpose_caches(pair, 1)
            project(before, 2)
            quantise_wproj(pair, 3)
            mix(before, 2)
            project(before, 3)
            mix(before, 3)
            scale_caches(pair)

        LAST = len(PANELS) - 1

        def finish(panel, s):
            add_b_out(panel, s)
            if panel == LAST:
                store(panel, s, s + 1)
            elif s % 2 == 1:
                store(panel, s - 1, s + 1)

        for panel in range(LAST + 1):
            regroup_wout(panel, 0)
            if panel == 0:
                quantise_hidden(2)
            for pair in range(4):
                if pair < 3:
                    regroup_wout(panel, pair + 1)
                quantise_wout(panel, pair)
                if panel == 0:
                    project(3, pair)
                    mix(3, pair)
                else:
                    multiply_out(panel, pair)
                    for s in BESIDE[pair]:
                        finish(panel - 1, s)
            if panel == 0:
                quantise_hidden(3)
                for pair in range(4):
                    multiply_out(0, pair)
        for s in range(4):
            finish(LAST, s)
